import numpy as np
import ml_dtypes


def mxq(x, axis, fmt="e4m3"):
    dtype, down = {"e4m3": (ml_dtypes.float8_e4m3fn, 7), "e5m2": (ml_dtypes.float8_e5m2, 14)}[fmt]
    v = np.moveaxis(np.asarray(x, np.float32).astype(ml_dtypes.bfloat16).astype(np.float64), axis, -1)
    blocks = v.reshape(v.shape[:-1] + (-1, 32))
    amax = np.abs(blocks).max(-1, keepdims=True)
    byte = np.maximum(np.where(amax > 0, np.frexp(amax)[1] - 1 + 127, 0) - down, 1)
    scale = np.exp2(byte - 127.0)
    codes = (blocks / scale).astype(np.float32).astype(dtype).astype(np.float64)
    return np.moveaxis((codes * scale).reshape(v.shape), -1, axis)


BF16 = ml_dtypes.bfloat16


def bf(x):
    return np.asarray(x, np.float32).astype(BF16)


def f64(x):
    return np.asarray(x).astype(np.float64)


B, D, C = 12288, 512, 128
REACH_SCALE = 10.0
COS_SCALE = 16.0


def setup_inputs():
    return {"x": bf(np.random.standard_normal((B, D))),
            "infused_feature": bf(np.random.standard_normal((B, D)) * 0.2),
            "min_dist": bf(np.sqrt(2.0 * D) * np.random.uniform(0.7, 1.2, (B, 1))),
            "W_cos": bf(np.random.standard_normal((C, D)) * np.random.uniform(0.5, 1.5, (C, 1)) / np.sqrt(D))}


def reference(x, infused_feature, min_dist, W_cos):
    reachability = REACH_SCALE / f64(min_dist)
    feat = reachability * (f64(x) + f64(infused_feature))
    norm_x = np.sqrt((feat * feat).sum(1, keepdims=True))
    ex = (norm_x / (1.0 + norm_x)) * (feat / norm_x)
    w = f64(W_cos)
    ew = w / np.sqrt((w * w).sum(1, keepdims=True))
    return mxq(COS_SCALE * ex, 1, "e4m3") @ mxq(ew, 1, "e4m3").T

@@ -1,0 +1,205 @@
+from contextlib import ExitStack
+
+import concourse.mybir as mybir
+from concourse.masks import make_identity
+
+BF16 = mybir.dt.bfloat16
+F32 = mybir.dt.float32
+U32 = mybir.dt.uint32
+U8 = mybir.dt.uint8
+FP8X4 = mybir.dt.float8_e4m3fn_x4
+ACT = mybir.ActivationFunctionType
+ALU = mybir.AluOpType
+
+P = 128
+B, D, C = 12288, 512, 128
+KB = D // P
+NT = B // P
+FLOPS = 2 * B * D * C
+
+PIN = False
+SIZES = [4] * 24
+
+
+def tile_metaembedding_classifier_pb_t_kernel(tc, x, infused_feature, min_dist, W_cos, out):
+    nc = tc.nc
+    assert sum(SIZES) == NT
+    x_v = x.rearrange("(p j) d -> p j d", p=P)
+    i_v = infused_feature.rearrange("(p j) d -> p j d", p=P)
+    o_v = out.rearrange("(p j) c -> p j c", p=P)
+    md_v = min_dist.rearrange("(p j) o -> p (j o)", p=P)
+    chunks = []
+    j0 = 0
+    for size in SIZES:
+        chunks.append((j0, size))
+        j0 += size
+    n = len(chunks)
+
+    with ExitStack() as ctx:
+        if PIN:
+            ctx.enter_context(tc.manual_schedule())
+        const = ctx.enter_context(tc.tile_pool(name="const", bufs=1))
+        ld = ctx.enter_context(tc.tile_pool(name="ld", bufs=3))
+        sp = ctx.enter_context(tc.tile_pool(name="sp", bufs=3))
+        small = ctx.enter_context(tc.tile_pool(name="small", bufs=4))
+        work = ctx.enter_context(tc.tile_pool(name="work", bufs=2))
+        op = ctx.enter_context(tc.tile_pool(name="op", bufs=3))
+        ps_t = ctx.enter_context(tc.psum_pool(name="ps_t", bufs=4))
+        ps_o = ctx.enter_context(tc.psum_pool(name="ps_o", bufs=2))
+
+        st = {}
+
+        w_sb = const.tile([P, D], BF16, name="w_sb")
+        nc.sync.dma_start(out=w_sb[:], in_=W_cos)
+        md_sb = const.tile([P, NT], BF16, name="md_sb")
+        nc.sync.dma_start(out=md_sb[:], in_=md_v)
+
+        def load(k):
+            if k < 0 or k >= n:
+                return
+            j, t = chunks[k]
+            xt = ld.tile([P, t, D], BF16, name="xt", tag="xt")
+            nc.sync.dma_start(out=xt[:], in_=x_v[:, j:j + t, :])
+            it = ld.tile([P, t, D], BF16, name="it", tag="it")
+            nc.sync.dma_start(out=it[:], in_=i_v[:, j:j + t, :])
+            st[k] = {"x": xt, "i": it}
+
+        load(0)
+        load(1)
+
+        one = const.tile([P, 1], F32, name="one")
+        nc.vector.memset(one[:], 1.0)
+        warm = const.tile([P, 1], F32, name="warm")
+        nc.scalar.activation(out=warm[:], in_=one[:], func=ACT.Sqrt)
+        ident = const.tile([P, P], BF16, name="ident")
+        make_identity(nc, ident[:])
+
+        md160 = const.tile([P, NT], F32, name="md160")
+        nc.vector.tensor_scalar(out=md160[:], in0=md_sb[:], scalar1=1.0 / 160.0, scalar2=None, op0=ALU.mult)
+
+        junk_w = work.tile([P, D], BF16, name="junk_w", tag="junk")
+        ssw = const.tile([P, 1], F32, name="ssw")
+        nc.scalar.activation(out=junk_w[:], in_=w_sb[:], func=ACT.Square, accum_out=ssw[:])
+        nw = const.tile([P, 1], F32, name="nw")
+        nc.scalar.activation(out=nw[:], in_=ssw[:], func=ACT.Sqrt)
+        rw = const.tile([P, 1], F32, name="rw")
+        nc.vector.reciprocal(out=rw[:], in_=nw[:])
+        ew = const.tile([P, D], BF16, name="ew")
+        nc.vector.tensor_scalar(out=ew[:], in0=w_sb[:], scalar1=rw[:, 0:1], scalar2=None, op0=ALU.mult)
+        tpw = ps_t.tile([P, 2, KB, P], BF16, name="tpw", tag="tp")
+        for b in range(KB):
+            nc.tensor.transpose(tpw[:, 0, b, :], ew[:, b * P:(b + 1) * P], ident[:])
+        gw = const.tile([P, P, KB], BF16, name="gw", align_bytes=64)
+        nc.scalar.copy(out=gw[:], in_=tpw[:, 0, :, :].rearrange("p b r -> p r b"))
+        w_codes = const.tile([P, C], U32, name="w_codes", align_bytes=64)
+        w_scales = const.tile([P, C], U8, name="w_scales", align_bytes=64)
+
+        def quant_w():
+            nc.vector.quantize_mx(
+                out=w_codes[:].bitcast(FP8X4), scales=w_scales[:], in_=gw[:].rearrange("p r b -> p (r b)")
+            )
+
+        def add(k):
+            if k < 0 or k >= n:
+                return
+            j, t = chunks[k]
+            s = sp.tile([P, t, D], F32, name="s", tag="s")
+            nc.vector.tensor_tensor(
+                out=s[:].rearrange("p t d -> p (t d)"),
+                in0=st[k]["x"][:].rearrange("p t d -> p (t d)"),
+                in1=st[k]["i"][:].rearrange("p t d -> p (t d)"),
+                op=ALU.add,
+            )
+            st[k]["s"] = s
+
+        def squares(k):
+            if k < 0 or k >= n:
+                return
+            j, t = chunks[k]
+            ss = small.tile([P, t], F32, name="ss", tag="ss")
+            for u in range(t):
+                junk = work.tile([P, D], BF16, name="junk", tag="junk")
+                nc.scalar.activation(out=junk[:], in_=st[k]["s"][:, u, :], func=ACT.Square, accum_out=ss[:, u:u + 1])
+            st[k]["ss"] = ss
+
+        def root(k):
+            if k < 0 or k >= n:
+                return
+            j, t = chunks[k]
+            q = small.tile([P, t], F32, name="q", tag="q")
+            nc.scalar.activation(out=q[:], in_=st[k]["ss"][:], func=ACT.Sqrt, scale=1.0 / 256.0)
+            st[k]["q"] = q
+
+        def scale_and_transpose(k):
+            if k < 0 or k >= n:
+                return
+            j, t = chunks[k]
+            dn = small.tile([P, t], F32, name="dn", tag="dn")
+            nc.vector.tensor_tensor(out=dn[:], in0=st[k]["q"][:], in1=md160[:, j:j + t], op=ALU.add)
+            f = small.tile([P, t], F32, name="f", tag="f")
+            nc.vector.reciprocal(out=f[:], in_=dn[:])
+            y = work.tile([P, t, D], BF16, name="y", tag="y")
+            for u in range(t):
+                nc.vector.tensor_scalar(
+                    out=y[:, u, :], in0=st[k]["s"][:, u, :], scalar1=f[:, u:u + 1], scalar2=None, op0=ALU.mult
+                )
+            banks = []
+            for u0 in range(0, t, 2):
+                w = min(2, t - u0)
+                tp = ps_t.tile([P, 2, KB, P], BF16, name="tp", tag="tp")
+                for u in range(w):
+                    for b in range(KB):
+                        nc.tensor.transpose(tp[:, u, b, :], y[:, u0 + u, b * P:(b + 1) * P], ident[:])
+                banks.append((u0, w, tp))
+            st[k]["banks"] = banks
+
+        def regroup(k):
+            if k < 0 or k >= n:
+                return
+            j, t = chunks[k]
+            g = work.tile([P, t, P, KB], BF16, name="g", tag="g", align_bytes=64)
+            for u0, w, tp in st[k]["banks"]:
+                nc.scalar.copy(out=g[:, u0:u0 + w, :, :], in_=tp[:, 0:w, :, :].rearrange("p u b r -> p u r b"))
+            st[k]["g"] = g
+
+        def quant_and_multiply(k):
+            if k < 0 or k >= n:
+                return
+            j, t = chunks[k]
+            codes = work.tile([P, t * P], U32, name="codes", tag="codes", align_bytes=64)
+            scales = work.tile([P, t * P], U8, name="scales", tag="scales", align_bytes=64)
+            nc.vector.quantize_mx(
+                out=codes[:].bitcast(FP8X4), scales=scales[:], in_=st[k]["g"][:].rearrange("p t r b -> p (t r b)")
+            )
+            acc = ps_o.tile([P, 4, C], F32, name="acc", tag="acc")
+            for u in range(t):
+                nc.tensor.matmul_mx(
+                    out=acc[:, u, :],
+                    lhsT=codes[:, u * P:(u + 1) * P].bitcast(FP8X4),
+                    lhsT_scale=scales[:, u * P:(u + 1) * P],
+                    rhs=w_codes[:].bitcast(FP8X4),
+                    rhs_scale=w_scales[:],
+                    start=True,
+                    stop=True,
+                )
+            st[k]["acc"] = acc
+
+        def store(k):
+            if k < 0 or k >= n:
+                return
+            j, t = chunks[k]
+            o = op.tile([P, t, C], F32, name="o", tag="o")
+            nc.vector.tensor_copy(out=o[:], in_=st[k]["acc"][:, 0:t, :])
+            nc.sync.dma_start(out=o_v[:, j:j + t, :], in_=o[:])
+
+        for k in range(-1, n + 4):
+            load(k + 3)
+            root(k - 1)
+            add(k + 1)
+            if k == 0:
+                quant_w()
+            regroup(k - 2)
+            scale_and_transpose(k - 1)
+            squares(k)
+            quant_and_multiply(k - 2)
+            store(k - 3)

@@ -17,7 +17,7 @@ KB = D // P
 NT = B // P
 FLOPS = 2 * B * D * C
 
-PIN = False
+PIN = True
 SIZES = [4] * 24
 
 

@@ -99,18 +99,22 @@ def tile_metaembedding_classifier_pb_t_kernel(tc, x, infused_feature, min_dist, 
                 out=w_codes[:].bitcast(FP8X4), scales=w_scales[:], in_=gw[:].rearrange("p r b -> p (r b)")
             )
 
-        def add(k):
+        def add(k, half):
             if k < 0 or k >= n:
                 return
             j, t = chunks[k]
-            s = sp.tile([P, t, D], F32, name="s", tag="s")
+            if half == 0:
+                st[k]["s"] = sp.tile([P, t, D], F32, name="s", tag="s")
+            h = (t + 1) // 2
+            lo, hi = (0, h) if half == 0 else (h, t)
+            if lo == hi:
+                return
             nc.vector.tensor_tensor(
-                out=s[:].rearrange("p t d -> p (t d)"),
-                in0=st[k]["x"][:].rearrange("p t d -> p (t d)"),
-                in1=st[k]["i"][:].rearrange("p t d -> p (t d)"),
+                out=st[k]["s"][:, lo:hi, :].rearrange("p t d -> p (t d)"),
+                in0=st[k]["x"][:, lo:hi, :].rearrange("p t d -> p (t d)"),
+                in1=st[k]["i"][:, lo:hi, :].rearrange("p t d -> p (t d)"),
                 op=ALU.add,
             )
-            st[k]["s"] = s
 
         def squares(k):
             if k < 0 or k >= n:
@@ -130,14 +134,27 @@ def tile_metaembedding_classifier_pb_t_kernel(tc, x, infused_feature, min_dist, 
             nc.scalar.activation(out=q[:], in_=st[k]["ss"][:], func=ACT.Sqrt, scale=1.0 / 256.0)
             st[k]["q"] = q
 
-        def scale_and_transpose(k):
+        def denom(k):
             if k < 0 or k >= n:
                 return
             j, t = chunks[k]
             dn = small.tile([P, t], F32, name="dn", tag="dn")
             nc.vector.tensor_tensor(out=dn[:], in0=st[k]["q"][:], in1=md160[:, j:j + t], op=ALU.add)
+            st[k]["dn"] = dn
+
+        def recip(k):
+            if k < 0 or k >= n:
+                return
+            j, t = chunks[k]
             f = small.tile([P, t], F32, name="f", tag="f")
-            nc.vector.reciprocal(out=f[:], in_=dn[:])
+            nc.vector.reciprocal(out=f[:], in_=st[k]["dn"][:])
+            st[k]["f"] = f
+
+        def scale_and_transpose(k):
+            if k < 0 or k >= n:
+                return
+            j, t = chunks[k]
+            f = st[k]["f"]
             y = work.tile([P, t, D], BF16, name="y", tag="y")
             for u in range(t):
                 nc.vector.tensor_scalar(
@@ -192,14 +209,17 @@ def tile_metaembedding_classifier_pb_t_kernel(tc, x, infused_feature, min_dist, 
             nc.vector.tensor_copy(out=o[:], in_=st[k]["acc"][:, 0:t, :])
             nc.sync.dma_start(out=o_v[:, j:j + t, :], in_=o[:])
 
-        for k in range(-1, n + 4):
+        for k in range(-1, n + 5):
+            store(k - 4)
             load(k + 3)
             root(k - 1)
-            add(k + 1)
+            add(k + 1, 0)
+            denom(k - 1)
+            add(k + 1, 1)
+            recip(k - 1)
             if k == 0:
                 quant_w()
-            regroup(k - 2)
-            scale_and_transpose(k - 1)
             squares(k)
-            quant_and_multiply(k - 2)
-            store(k - 3)
+            quant_and_multiply(k - 3)
+            scale_and_transpose(k - 1)
+            regroup(k - 2)

@@ -10,34 +10,29 @@ U8 = mybir.dt.uint8
 FP8X4 = mybir.dt.float8_e4m3fn_x4
 ACT = mybir.ActivationFunctionType
 ALU = mybir.AluOpType
+AX = mybir.AxisListType
 
 P = 128
 B, D, C = 12288, 512, 128
-KB = D // P
 NT = B // P
+HD = D // 2
+R = P // 2
+T = 4
+LG = 8
 FLOPS = 2 * B * D * C
-
-PIN = True
-SIZES = [4] * 24
 
 
 def tile_metaembedding_classifier_pb_t_kernel(tc, x, infused_feature, min_dist, W_cos, out):
     nc = tc.nc
-    assert sum(SIZES) == NT
-    x_v = x.rearrange("(p j) d -> p j d", p=P)
-    i_v = infused_feature.rearrange("(p j) d -> p j d", p=P)
+    x_v = x.rearrange("(r h j) (u d) -> u h r j d", r=R, h=2, u=2)
+    i_v = infused_feature.rearrange("(r h j) (u d) -> u h r j d", r=R, h=2, u=2)
     o_v = out.rearrange("(p j) c -> p j c", p=P)
-    md_v = min_dist.rearrange("(p j) o -> p (j o)", p=P)
-    chunks = []
-    j0 = 0
-    for size in SIZES:
-        chunks.append((j0, size))
-        j0 += size
-    n = len(chunks)
+    md_v = min_dist.rearrange("(r g) o -> r (g o)", r=R)
+    n = NT // T
+    ng = NT // LG
 
     with ExitStack() as ctx:
-        if PIN:
-            ctx.enter_context(tc.manual_schedule())
+        ctx.enter_context(tc.manual_schedule())
         const = ctx.enter_context(tc.tile_pool(name="const", bufs=1))
         ld = ctx.enter_context(tc.tile_pool(name="ld", bufs=3))
         sp = ctx.enter_context(tc.tile_pool(name="sp", bufs=3))
@@ -46,26 +41,34 @@ def tile_metaembedding_classifier_pb_t_kernel(tc, x, infused_feature, min_dist, 
         op = ctx.enter_context(tc.tile_pool(name="op", bufs=3))
         ps_t = ctx.enter_context(tc.psum_pool(name="ps_t", bufs=4))
         ps_o = ctx.enter_context(tc.psum_pool(name="ps_o", bufs=2))
+        ps_p = ctx.enter_context(tc.psum_pool(name="ps_p", bufs=2))
 
         st = {}
+        groups = {}
 
+        def load(g, pieces):
+            if g < 0 or g >= ng:
+                return
+            xt = ld.tile([P, 2, LG, HD], BF16, name="xt", tag="xt")
+            it = ld.tile([P, 2, LG, HD], BF16, name="it", tag="it")
+            step = LG // pieces
+            for a in range(0, LG, step):
+                for h in range(2):
+                    for dst, src in ((xt, x_v), (it, i_v)):
+                        for u in range(2):
+                            nc.sync.dma_start(
+                                out=dst[u:P:2, h, a:a + step, :],
+                                in_=src[u, h, :, g * LG + a:g * LG + a + step, :],
+                            )
+            groups[g] = (xt, it)
+
+        load(0, 2)
         w_sb = const.tile([P, D], BF16, name="w_sb")
         nc.sync.dma_start(out=w_sb[:], in_=W_cos)
-        md_sb = const.tile([P, NT], BF16, name="md_sb")
-        nc.sync.dma_start(out=md_sb[:], in_=md_v)
-
-        def load(k):
-            if k < 0 or k >= n:
-                return
-            j, t = chunks[k]
-            xt = ld.tile([P, t, D], BF16, name="xt", tag="xt")
-            nc.sync.dma_start(out=xt[:], in_=x_v[:, j:j + t, :])
-            it = ld.tile([P, t, D], BF16, name="it", tag="it")
-            nc.sync.dma_start(out=it[:], in_=i_v[:, j:j + t, :])
-            st[k] = {"x": xt, "i": it}
-
-        load(0)
-        load(1)
+        md_sb = const.tile([P, 2 * NT], BF16, name="md_sb")
+        for u in range(2):
+            nc.sync.dma_start(out=md_sb[u:P:2, :], in_=md_v)
+        load(1, 1)
 
         one = const.tile([P, 1], F32, name="one")
         nc.vector.memset(one[:], 1.0)
@@ -73,9 +76,19 @@ def tile_metaembedding_classifier_pb_t_kernel(tc, x, infused_feature, min_dist, 
         nc.scalar.activation(out=warm[:], in_=one[:], func=ACT.Sqrt)
         ident = const.tile([P, P], BF16, name="ident")
         make_identity(nc, ident[:])
+        ident32 = const.tile([P, P], F32, name="ident32")
+        make_identity(nc, ident32[:])
+        pair_half = const.tile([P, R], F32, name="pair_half")
+        nc.vector.tensor_reduce(
+            out=pair_half[:], in_=ident32[:].rearrange("p (a b) -> p a b", b=2), axis=AX.X, op=ALU.add
+        )
+        pair = const.tile([P, R, 2], F32, name="pair")
+        nc.vector.tensor_copy(out=pair[:], in_=pair_half[:].unsqueeze(2).to_broadcast([P, R, 2]))
 
-        md160 = const.tile([P, NT], F32, name="md160")
-        nc.vector.tensor_scalar(out=md160[:], in0=md_sb[:], scalar1=1.0 / 160.0, scalar2=None, op0=ALU.mult)
+        md160 = const.tile([P, 2, NT], F32, name="md160")
+        nc.vector.tensor_scalar(
+            out=md160[:].rearrange("p h j -> p (h j)"), in0=md_sb[:], scalar1=1.0 / 160.0, scalar2=None, op0=ALU.mult
+        )
 
         junk_w = work.tile([P, D], BF16, name="junk_w", tag="junk")
         ssw = const.tile([P, 1], F32, name="ssw")
@@ -86,114 +99,119 @@ def tile_metaembedding_classifier_pb_t_kernel(tc, x, infused_feature, min_dist, 
         nc.vector.reciprocal(out=rw[:], in_=nw[:])
         ew = const.tile([P, D], BF16, name="ew")
         nc.vector.tensor_scalar(out=ew[:], in0=w_sb[:], scalar1=rw[:, 0:1], scalar2=None, op0=ALU.mult)
-        tpw = ps_t.tile([P, 2, KB, P], BF16, name="tpw", tag="tp")
-        for b in range(KB):
-            nc.tensor.transpose(tpw[:, 0, b, :], ew[:, b * P:(b + 1) * P], ident[:])
-        gw = const.tile([P, P, KB], BF16, name="gw", align_bytes=64)
-        nc.scalar.copy(out=gw[:], in_=tpw[:, 0, :, :].rearrange("p b r -> p r b"))
+        tpw = ps_t.tile([P, 8, P], BF16, name="tpw", tag="tp")
+        for b in range(4):
+            nc.tensor.transpose(tpw[:, b, :], ew[:, b * P:(b + 1) * P], ident[:])
+        gw = const.tile([P, P, 2, 2], BF16, name="gw", align_bytes=64)
+        nc.scalar.copy(out=gw[:], in_=tpw[:, 0:4, :].rearrange("p (u v) c -> p c v u", u=2))
         w_codes = const.tile([P, C], U32, name="w_codes", align_bytes=64)
         w_scales = const.tile([P, C], U8, name="w_scales", align_bytes=64)
 
         def quant_w():
             nc.vector.quantize_mx(
-                out=w_codes[:].bitcast(FP8X4), scales=w_scales[:], in_=gw[:].rearrange("p r b -> p (r b)")
+                out=w_codes[:].bitcast(FP8X4), scales=w_scales[:], in_=gw[:].rearrange("p c v u -> p (c v u)")
             )
 
-        def add(k, half):
-            if k < 0 or k >= n:
+        def ok(k):
+            return 0 <= k < n
+
+        def add(k, h):
+            if not ok(k):
                 return
-            j, t = chunks[k]
-            if half == 0:
-                st[k]["s"] = sp.tile([P, t, D], F32, name="s", tag="s")
-            h = (t + 1) // 2
-            lo, hi = (0, h) if half == 0 else (h, t)
-            if lo == hi:
-                return
+            if h == 0:
+                st[k] = {"s": sp.tile([P, 2, T, HD], F32, name="s", tag="s")}
+            xt, it = groups[(k * T) // LG]
+            a = (k * T) % LG
             nc.vector.tensor_tensor(
-                out=st[k]["s"][:, lo:hi, :].rearrange("p t d -> p (t d)"),
-                in0=st[k]["x"][:, lo:hi, :].rearrange("p t d -> p (t d)"),
-                in1=st[k]["i"][:, lo:hi, :].rearrange("p t d -> p (t d)"),
+                out=st[k]["s"][:, h, :, :].rearrange("p t d -> p (t d)"),
+                in0=xt[:, h, a:a + T, :].rearrange("p t d -> p (t d)"),
+                in1=it[:, h, a:a + T, :].rearrange("p t d -> p (t d)"),
                 op=ALU.add,
             )
 
         def squares(k):
-            if k < 0 or k >= n:
+            if not ok(k):
                 return
-            j, t = chunks[k]
-            ss = small.tile([P, t], F32, name="ss", tag="ss")
-            for u in range(t):
-                junk = work.tile([P, D], BF16, name="junk", tag="junk")
-                nc.scalar.activation(out=junk[:], in_=st[k]["s"][:, u, :], func=ACT.Square, accum_out=ss[:, u:u + 1])
-            st[k]["ss"] = ss
+            ssh = small.tile([P, 2, T], F32, name="ssh", tag="ssh")
+            for h in range(2):
+                for t in range(T):
+                    junk = work.tile([P, HD], BF16, name="junk", tag="junk")
+                    nc.scalar.activation(
+                        out=junk[:], in_=st[k]["s"][:, h, t, :], func=ACT.Square, accum_out=ssh[:, h, t:t + 1]
+                    )
+            pr = ps_p.tile([P, 2 * T], F32, name="pr", tag="pr")
+            nc.tensor.matmul(
+                out=pr[:],
+                lhsT=pair[:].rearrange("p a b -> p (a b)"),
+                rhs=ssh[:].rearrange("p h t -> p (h t)"),
+                start=True,
+                stop=True,
+            )
+            st[k]["pr"] = pr
 
         def root(k):
-            if k < 0 or k >= n:
+            if not ok(k):
                 return
-            j, t = chunks[k]
-            q = small.tile([P, t], F32, name="q", tag="q")
-            nc.scalar.activation(out=q[:], in_=st[k]["ss"][:], func=ACT.Sqrt, scale=1.0 / 256.0)
+            q = small.tile([P, 2, T], F32, name="q", tag="q")
+            nc.scalar.activation(
+                out=q[:].rearrange("p h t -> p (h t)"), in_=st[k]["pr"][:], func=ACT.Sqrt, scale=1.0 / 256.0
+            )
             st[k]["q"] = q
 
         def denom(k):
-            if k < 0 or k >= n:
+            if not ok(k):
                 return
-            j, t = chunks[k]
-            dn = small.tile([P, t], F32, name="dn", tag="dn")
-            nc.vector.tensor_tensor(out=dn[:], in0=st[k]["q"][:], in1=md160[:, j:j + t], op=ALU.add)
+            dn = small.tile([P, 2, T], F32, name="dn", tag="dn")
+            nc.vector.tensor_tensor(out=dn[:], in0=st[k]["q"][:], in1=md160[:, :, k * T:(k + 1) * T], op=ALU.add)
             st[k]["dn"] = dn
 
         def recip(k):
-            if k < 0 or k >= n:
+            if not ok(k):
                 return
-            j, t = chunks[k]
-            f = small.tile([P, t], F32, name="f", tag="f")
+            f = small.tile([P, 2, T], F32, name="f", tag="f")
             nc.vector.reciprocal(out=f[:], in_=st[k]["dn"][:])
             st[k]["f"] = f
 
         def scale_and_transpose(k):
-            if k < 0 or k >= n:
+            if not ok(k):
                 return
-            j, t = chunks[k]
             f = st[k]["f"]
-            y = work.tile([P, t, D], BF16, name="y", tag="y")
-            for u in range(t):
-                nc.vector.tensor_scalar(
-                    out=y[:, u, :], in0=st[k]["s"][:, u, :], scalar1=f[:, u:u + 1], scalar2=None, op0=ALU.mult
-                )
+            y = work.tile([P, 2, T, HD], BF16, name="y", tag="y")
+            for t in range(T):
+                for h in range(2):
+                    nc.vector.tensor_scalar(
+                        out=y[:, h, t, :], in0=st[k]["s"][:, h, t, :], scalar1=f[:, h, t:t + 1], scalar2=None, op0=ALU.mult
+                    )
             banks = []
-            for u0 in range(0, t, 2):
-                w = min(2, t - u0)
-                tp = ps_t.tile([P, 2, KB, P], BF16, name="tp", tag="tp")
-                for u in range(w):
-                    for b in range(KB):
-                        nc.tensor.transpose(tp[:, u, b, :], y[:, u0 + u, b * P:(b + 1) * P], ident[:])
-                banks.append((u0, w, tp))
+            for t0 in range(0, T, 2):
+                tp = ps_t.tile([P, 2, R, 2, 2, 2], BF16, name="tp", tag="tp")
+                for e in range(2):
+                    for h in range(2):
+                        for v in range(2):
+                            nc.tensor.transpose(tp[:, e, :, h, v, :], y[:, h, t0 + e, v * P:(v + 1) * P], ident[:])
+                banks.append(tp)
             st[k]["banks"] = banks
 
-        def regroup(k):
-            if k < 0 or k >= n:
+        def copy_banks(k):
+            if not ok(k):
                 return
-            j, t = chunks[k]
-            g = work.tile([P, t, P, KB], BF16, name="g", tag="g", align_bytes=64)
-            for u0, w, tp in st[k]["banks"]:
-                nc.scalar.copy(out=g[:, u0:u0 + w, :, :], in_=tp[:, 0:w, :, :].rearrange("p u b r -> p u r b"))
+            g = work.tile([P, T * D], BF16, name="g", tag="g", align_bytes=64)
+            for i, tp in enumerate(st[k]["banks"]):
+                nc.scalar.copy(out=g[:, i * 2 * D:(i + 1) * 2 * D], in_=tp[:].rearrange("p e r h v u -> p (e r h v u)"))
             st[k]["g"] = g
 
         def quant_and_multiply(k):
-            if k < 0 or k >= n:
+            if not ok(k):
                 return
-            j, t = chunks[k]
-            codes = work.tile([P, t * P], U32, name="codes", tag="codes", align_bytes=64)
-            scales = work.tile([P, t * P], U8, name="scales", tag="scales", align_bytes=64)
-            nc.vector.quantize_mx(
-                out=codes[:].bitcast(FP8X4), scales=scales[:], in_=st[k]["g"][:].rearrange("p t r b -> p (t r b)")
-            )
-            acc = ps_o.tile([P, 4, C], F32, name="acc", tag="acc")
-            for u in range(t):
+            codes = work.tile([P, T * P], U32, name="codes", tag="codes", align_bytes=64)
+            scales = work.tile([P, T * P], U8, name="scales", tag="scales", align_bytes=64)
+            nc.vector.quantize_mx(out=codes[:].bitcast(FP8X4), scales=scales[:], in_=st[k]["g"][:])
+            acc = ps_o.tile([P, T, C], F32, name="acc", tag="acc")
+            for t in range(T):
                 nc.tensor.matmul_mx(
-                    out=acc[:, u, :],
-                    lhsT=codes[:, u * P:(u + 1) * P].bitcast(FP8X4),
-                    lhsT_scale=scales[:, u * P:(u + 1) * P],
+                    out=acc[:, t, :],
+                    lhsT=codes[:, t * P:(t + 1) * P].bitcast(FP8X4),
+                    lhsT_scale=scales[:, t * P:(t + 1) * P],
                     rhs=w_codes[:].bitcast(FP8X4),
                     rhs_scale=w_scales[:],
                     start=True,
@@ -202,16 +220,15 @@ def tile_metaembedding_classifier_pb_t_kernel(tc, x, infused_feature, min_dist, 
             st[k]["acc"] = acc
 
         def store(k):
-            if k < 0 or k >= n:
+            if not ok(k):
                 return
-            j, t = chunks[k]
-            o = op.tile([P, t, C], F32, name="o", tag="o")
-            nc.vector.tensor_copy(out=o[:], in_=st[k]["acc"][:, 0:t, :])
-            nc.sync.dma_start(out=o_v[:, j:j + t, :], in_=o[:])
+            o = op.tile([P, T, C], F32, name="o", tag="o")
+            nc.scalar.copy(out=o[:], in_=st[k]["acc"][:])
+            nc.sync.dma_start(out=o_v[:, k * T:(k + 1) * T, :], in_=o[:])
 
         for k in range(-1, n + 5):
-            store(k - 4)
-            load(k + 3)
+            if k % 2 == 1:
+                load((k + 5) // 2, 1)
             root(k - 1)
             add(k + 1, 0)
             denom(k - 1)
@@ -222,4 +239,5 @@ def tile_metaembedding_classifier_pb_t_kernel(tc, x, infused_feature, min_dist, 
             squares(k)
             quant_and_multiply(k - 3)
             scale_and_transpose(k - 1)
-            regroup(k - 2)
+            copy_banks(k - 2)
+            store(k - 4)

@@ -53,6 +53,8 @@ def tile_metaembedding_classifier_pb_t_kernel(tc, x, infused_feature, min_dist, 
             it = ld.tile([P, 2, LG, HD], BF16, name="it", tag="it")
             step = LG // pieces
             for a in range(0, LG, step):
+                if g == 0 and a == step:
+                    load_small()
                 for h in range(2):
                     for dst, src in ((xt, x_v), (it, i_v)):
                         for u in range(2):
@@ -62,12 +64,15 @@ def tile_metaembedding_classifier_pb_t_kernel(tc, x, infused_feature, min_dist, 
                             )
             groups[g] = (xt, it)
 
-        load(0, 2)
         w_sb = const.tile([P, D], BF16, name="w_sb")
-        nc.sync.dma_start(out=w_sb[:], in_=W_cos)
         md_sb = const.tile([P, 2 * NT], BF16, name="md_sb")
-        for u in range(2):
-            nc.sync.dma_start(out=md_sb[u:P:2, :], in_=md_v)
+
+        def load_small():
+            for u in range(2):
+                nc.sync.dma_start(out=md_sb[u:P:2, :], in_=md_v)
+            nc.sync.dma_start(out=w_sb[:], in_=W_cos)
+
+        load(0, 2)
         load(1, 1)
 
         one = const.tile([P, 1], F32, name="one")
@@ -86,24 +91,38 @@ def tile_metaembedding_classifier_pb_t_kernel(tc, x, infused_feature, min_dist, 
         nc.vector.tensor_copy(out=pair[:], in_=pair_half[:].unsqueeze(2).to_broadcast([P, R, 2]))
 
         md160 = const.tile([P, 2, NT], F32, name="md160")
-        nc.vector.tensor_scalar(
-            out=md160[:].rearrange("p h j -> p (h j)"), in0=md_sb[:], scalar1=1.0 / 160.0, scalar2=None, op0=ALU.mult
-        )
-
-        junk_w = work.tile([P, D], BF16, name="junk_w", tag="junk")
         ssw = const.tile([P, 1], F32, name="ssw")
-        nc.scalar.activation(out=junk_w[:], in_=w_sb[:], func=ACT.Square, accum_out=ssw[:])
         nw = const.tile([P, 1], F32, name="nw")
-        nc.scalar.activation(out=nw[:], in_=ssw[:], func=ACT.Sqrt)
         rw = const.tile([P, 1], F32, name="rw")
-        nc.vector.reciprocal(out=rw[:], in_=nw[:])
         ew = const.tile([P, D], BF16, name="ew")
-        nc.vector.tensor_scalar(out=ew[:], in0=w_sb[:], scalar1=rw[:, 0:1], scalar2=None, op0=ALU.mult)
-        tpw = ps_t.tile([P, 8, P], BF16, name="tpw", tag="tp")
-        for b in range(4):
-            nc.tensor.transpose(tpw[:, b, :], ew[:, b * P:(b + 1) * P], ident[:])
         gw = const.tile([P, P, 2, 2], BF16, name="gw", align_bytes=64)
-        nc.scalar.copy(out=gw[:], in_=tpw[:, 0:4, :].rearrange("p (u v) c -> p c v u", u=2))
+        wst = {}
+
+        def scale_md():
+            nc.vector.tensor_scalar(
+                out=md160[:].rearrange("p h j -> p (h j)"), in0=md_sb[:], scalar1=1.0 / 160.0, scalar2=None, op0=ALU.mult
+            )
+
+        def w_square():
+            junk_w = work.tile([P, D], BF16, name="junk_w", tag="junk")
+            nc.scalar.activation(out=junk_w[:], in_=w_sb[:], func=ACT.Square, accum_out=ssw[:])
+
+        def w_root():
+            nc.scalar.activation(out=nw[:], in_=ssw[:], func=ACT.Sqrt)
+
+        def w_recip():
+            nc.vector.reciprocal(out=rw[:], in_=nw[:])
+
+        def w_scale_and_transpose():
+            nc.vector.tensor_scalar(out=ew[:], in0=w_sb[:], scalar1=rw[:, 0:1], scalar2=None, op0=ALU.mult)
+            tpw = ps_t.tile([P, 8, P], BF16, name="tpw", tag="tp")
+            for b in range(4):
+                nc.tensor.transpose(tpw[:, b, :], ew[:, b * P:(b + 1) * P], ident[:])
+            wst["tpw"] = tpw
+
+        def w_copy():
+            nc.scalar.copy(out=gw[:], in_=wst["tpw"][:, 0:4, :].rearrange("p (u v) c -> p c v u", u=2))
+
         w_codes = const.tile([P, C], U32, name="w_codes", align_bytes=64)
         w_scales = const.tile([P, C], U8, name="w_scales", align_bytes=64)
 
@@ -223,21 +242,36 @@ def tile_metaembedding_classifier_pb_t_kernel(tc, x, infused_feature, min_dist, 
             if not ok(k):
                 return
             o = op.tile([P, T, C], F32, name="o", tag="o")
-            nc.scalar.copy(out=o[:], in_=st[k]["acc"][:])
+            if k % 2 == 1:
+                nc.vector.tensor_copy(out=o[:], in_=st[k]["acc"][:])
+            else:
+                nc.scalar.copy(out=o[:], in_=st[k]["acc"][:])
             nc.sync.dma_start(out=o_v[:, k * T:(k + 1) * T, :], in_=o[:])
 
         for k in range(-1, n + 5):
             if k % 2 == 1:
                 load((k + 5) // 2, 1)
             root(k - 1)
+            if k == 1:
+                w_root()
             add(k + 1, 0)
             denom(k - 1)
+            if k == 1:
+                w_recip()
             add(k + 1, 1)
             recip(k - 1)
             if k == 0:
+                scale_md()
+            if k == 1:
+                w_scale_and_transpose()
+            if k == 2:
                 quant_w()
             squares(k)
+            if k == 0:
+                w_square()
             quant_and_multiply(k - 3)
             scale_and_transpose(k - 1)
             copy_banks(k - 2)
+            if k == 1:
+                w_copy()
             store(k - 4)

@@ -10,70 +10,63 @@ U8 = mybir.dt.uint8
 FP8X4 = mybir.dt.float8_e4m3fn_x4
 ACT = mybir.ActivationFunctionType
 ALU = mybir.AluOpType
-AX = mybir.AxisListType
 
 P = 128
 B, D, C = 12288, 512, 128
+KB = D // P
 NT = B // P
-HD = D // 2
-R = P // 2
-T = 4
-LG = 8
 FLOPS = 2 * B * D * C
+
+PIN = True
+SIZES = [4] * 24
 
 
 def tile_metaembedding_classifier_pb_t_kernel(tc, x, infused_feature, min_dist, W_cos, out):
     nc = tc.nc
-    x_v = x.rearrange("(r h j) (u d) -> u h r j d", r=R, h=2, u=2)
-    i_v = infused_feature.rearrange("(r h j) (u d) -> u h r j d", r=R, h=2, u=2)
+    assert sum(SIZES) == NT
+    x_v = x.rearrange("(p j) d -> p j d", p=P)
+    i_v = infused_feature.rearrange("(p j) d -> p j d", p=P)
     o_v = out.rearrange("(p j) c -> p j c", p=P)
-    md_v = min_dist.rearrange("(r g) o -> r (g o)", r=R)
-    n = NT // T
-    ng = NT // LG
+    md_v = min_dist.rearrange("(p j) o -> p (j o)", p=P)
+    chunks = []
+    j0 = 0
+    for size in SIZES:
+        chunks.append((j0, size))
+        j0 += size
+    n = len(chunks)
 
     with ExitStack() as ctx:
-        ctx.enter_context(tc.manual_schedule())
+        if PIN:
+            ctx.enter_context(tc.manual_schedule())
         const = ctx.enter_context(tc.tile_pool(name="const", bufs=1))
-        ld = ctx.enter_context(tc.tile_pool(name="ld", bufs=3))
-        sp = ctx.enter_context(tc.tile_pool(name="sp", bufs=3))
-        small = ctx.enter_context(tc.tile_pool(name="small", bufs=4))
-        work = ctx.enter_context(tc.tile_pool(name="work", bufs=2))
-        op = ctx.enter_context(tc.tile_pool(name="op", bufs=3))
-        ps_t = ctx.enter_context(tc.psum_pool(name="ps_t", bufs=4))
-        ps_o = ctx.enter_context(tc.psum_pool(name="ps_o", bufs=2))
-        ps_p = ctx.enter_context(tc.psum_pool(name="ps_p", bufs=2))
+        ld = ctx.enter_context(tc.tile_pool(name="ld", bufs=4))
+        sp = ctx.enter_context(tc.tile_pool(name="sp", bufs=4))
+        small = ctx.enter_context(tc.tile_pool(name="small", bufs=6))
+        work = ctx.enter_context(tc.tile_pool(name="work", bufs=3))
+        op = ctx.enter_context(tc.tile_pool(name="op", bufs=4))
+        ps_t = ctx.enter_context(tc.psum_pool(name="ps_t", bufs=5))
+        ps_o = ctx.enter_context(tc.psum_pool(name="ps_o", bufs=3))
 
         st = {}
-        groups = {}
-
-        def load(g, pieces):
-            if g < 0 or g >= ng:
-                return
-            xt = ld.tile([P, 2, LG, HD], BF16, name="xt", tag="xt")
-            it = ld.tile([P, 2, LG, HD], BF16, name="it", tag="it")
-            step = LG // pieces
-            for a in range(0, LG, step):
-                if g == 0 and a == step:
-                    load_small()
-                for h in range(2):
-                    for dst, src in ((xt, x_v), (it, i_v)):
-                        for u in range(2):
-                            nc.sync.dma_start(
-                                out=dst[u:P:2, h, a:a + step, :],
-                                in_=src[u, h, :, g * LG + a:g * LG + a + step, :],
-                            )
-            groups[g] = (xt, it)
 
         w_sb = const.tile([P, D], BF16, name="w_sb")
-        md_sb = const.tile([P, 2 * NT], BF16, name="md_sb")
+        nc.sync.dma_start(out=w_sb[:], in_=W_cos)
+        md_sb = const.tile([P, NT], BF16, name="md_sb")
+        nc.sync.dma_start(out=md_sb[:], in_=md_v)
 
-        def load_small():
-            for u in range(2):
-                nc.sync.dma_start(out=md_sb[u:P:2, :], in_=md_v)
-            nc.sync.dma_start(out=w_sb[:], in_=W_cos)
+        def load(k):
+            if k < 0 or k >= n:
+                return
+            j, t = chunks[k]
+            xt = ld.tile([P, t, D], BF16, name="xt", tag="xt")
+            nc.sync.dma_start(out=xt[:], in_=x_v[:, j:j + t, :])
+            it = ld.tile([P, t, D], BF16, name="it", tag="it")
+            nc.sync.dma_start(out=it[:], in_=i_v[:, j:j + t, :])
+            st[k] = {"x": xt, "i": it}
 
-        load(0, 2)
-        load(1, 1)
+        load(0)
+        load(1)
+        load(2)
 
         one = const.tile([P, 1], F32, name="one")
         nc.vector.memset(one[:], 1.0)
@@ -81,156 +74,127 @@ def tile_metaembedding_classifier_pb_t_kernel(tc, x, infused_feature, min_dist, 
         nc.scalar.activation(out=warm[:], in_=one[:], func=ACT.Sqrt)
         ident = const.tile([P, P], BF16, name="ident")
         make_identity(nc, ident[:])
-        ident32 = const.tile([P, P], F32, name="ident32")
-        make_identity(nc, ident32[:])
-        pair_half = const.tile([P, R], F32, name="pair_half")
-        nc.vector.tensor_reduce(
-            out=pair_half[:], in_=ident32[:].rearrange("p (a b) -> p a b", b=2), axis=AX.X, op=ALU.add
-        )
-        pair = const.tile([P, R, 2], F32, name="pair")
-        nc.vector.tensor_copy(out=pair[:], in_=pair_half[:].unsqueeze(2).to_broadcast([P, R, 2]))
 
-        md160 = const.tile([P, 2, NT], F32, name="md160")
+        md160 = const.tile([P, NT], F32, name="md160")
+        nc.vector.tensor_scalar(out=md160[:], in0=md_sb[:], scalar1=1.0 / 160.0, scalar2=None, op0=ALU.mult)
+
+        junk_w = work.tile([P, D], BF16, name="junk_w", tag="junk")
         ssw = const.tile([P, 1], F32, name="ssw")
+        nc.scalar.activation(out=junk_w[:], in_=w_sb[:], func=ACT.Square, accum_out=ssw[:])
         nw = const.tile([P, 1], F32, name="nw")
+        nc.scalar.activation(out=nw[:], in_=ssw[:], func=ACT.Sqrt)
         rw = const.tile([P, 1], F32, name="rw")
+        nc.vector.reciprocal(out=rw[:], in_=nw[:])
         ew = const.tile([P, D], BF16, name="ew")
-        gw = const.tile([P, P, 2, 2], BF16, name="gw", align_bytes=64)
-        wst = {}
-
-        def scale_md():
-            nc.vector.tensor_scalar(
-                out=md160[:].rearrange("p h j -> p (h j)"), in0=md_sb[:], scalar1=1.0 / 160.0, scalar2=None, op0=ALU.mult
-            )
-
-        def w_square():
-            junk_w = work.tile([P, D], BF16, name="junk_w", tag="junk")
-            nc.scalar.activation(out=junk_w[:], in_=w_sb[:], func=ACT.Square, accum_out=ssw[:])
-
-        def w_root():
-            nc.scalar.activation(out=nw[:], in_=ssw[:], func=ACT.Sqrt)
-
-        def w_recip():
-            nc.vector.reciprocal(out=rw[:], in_=nw[:])
-
-        def w_scale_and_transpose():
-            nc.vector.tensor_scalar(out=ew[:], in0=w_sb[:], scalar1=rw[:, 0:1], scalar2=None, op0=ALU.mult)
-            tpw = ps_t.tile([P, 8, P], BF16, name="tpw", tag="tp")
-            for b in range(4):
-                nc.tensor.transpose(tpw[:, b, :], ew[:, b * P:(b + 1) * P], ident[:])
-            wst["tpw"] = tpw
-
-        def w_copy():
-            nc.scalar.copy(out=gw[:], in_=wst["tpw"][:, 0:4, :].rearrange("p (u v) c -> p c v u", u=2))
-
+        nc.vector.tensor_scalar(out=ew[:], in0=w_sb[:], scalar1=rw[:, 0:1], scalar2=None, op0=ALU.mult)
+        tpw = ps_t.tile([P, 2, KB, P], BF16, name="tpw", tag="tp")
+        for b in range(KB):
+            nc.tensor.transpose(tpw[:, 0, b, :], ew[:, b * P:(b + 1) * P], ident[:])
+        gw = const.tile([P, P, KB], BF16, name="gw", align_bytes=64)
+        nc.scalar.copy(out=gw[:], in_=tpw[:, 0, :, :].rearrange("p b r -> p r b"))
         w_codes = const.tile([P, C], U32, name="w_codes", align_bytes=64)
         w_scales = const.tile([P, C], U8, name="w_scales", align_bytes=64)
 
         def quant_w():
             nc.vector.quantize_mx(
-                out=w_codes[:].bitcast(FP8X4), scales=w_scales[:], in_=gw[:].rearrange("p c v u -> p (c v u)")
+                out=w_codes[:].bitcast(FP8X4), scales=w_scales[:], in_=gw[:].rearrange("p r b -> p (r b)")
             )
 
-        def ok(k):
-            return 0 <= k < n
-
-        def add(k, h):
-            if not ok(k):
+        def add(k, half):
+            if k < 0 or k >= n:
                 return
-            if h == 0:
-                st[k] = {"s": sp.tile([P, 2, T, HD], F32, name="s", tag="s")}
-            xt, it = groups[(k * T) // LG]
-            a = (k * T) % LG
+            j, t = chunks[k]
+            if half == 0:
+                st[k]["s"] = sp.tile([P, t, D], F32, name="s", tag="s")
+            h = (t + 1) // 2
+            lo, hi = (0, h) if half == 0 else (h, t)
+            if lo == hi:
+                return
             nc.vector.tensor_tensor(
-                out=st[k]["s"][:, h, :, :].rearrange("p t d -> p (t d)"),
-                in0=xt[:, h, a:a + T, :].rearrange("p t d -> p (t d)"),
-                in1=it[:, h, a:a + T, :].rearrange("p t d -> p (t d)"),
+                out=st[k]["s"][:, lo:hi, :].rearrange("p t d -> p (t d)"),
+                in0=st[k]["x"][:, lo:hi, :].rearrange("p t d -> p (t d)"),
+                in1=st[k]["i"][:, lo:hi, :].rearrange("p t d -> p (t d)"),
                 op=ALU.add,
             )
 
         def squares(k):
-            if not ok(k):
+            if k < 0 or k >= n:
                 return
-            ssh = small.tile([P, 2, T], F32, name="ssh", tag="ssh")
-            for h in range(2):
-                for t in range(T):
-                    junk = work.tile([P, HD], BF16, name="junk", tag="junk")
-                    nc.scalar.activation(
-                        out=junk[:], in_=st[k]["s"][:, h, t, :], func=ACT.Square, accum_out=ssh[:, h, t:t + 1]
-                    )
-            pr = ps_p.tile([P, 2 * T], F32, name="pr", tag="pr")
-            nc.tensor.matmul(
-                out=pr[:],
-                lhsT=pair[:].rearrange("p a b -> p (a b)"),
-                rhs=ssh[:].rearrange("p h t -> p (h t)"),
-                start=True,
-                stop=True,
-            )
-            st[k]["pr"] = pr
+            j, t = chunks[k]
+            ss = small.tile([P, t], F32, name="ss", tag="ss")
+            for u in range(t):
+                junk = work.tile([P, D], BF16, name="junk", tag="junk")
+                nc.scalar.activation(out=junk[:], in_=st[k]["s"][:, u, :], func=ACT.Square, accum_out=ss[:, u:u + 1])
+            st[k]["ss"] = ss
 
         def root(k):
-            if not ok(k):
+            if k < 0 or k >= n:
                 return
-            q = small.tile([P, 2, T], F32, name="q", tag="q")
-            nc.scalar.activation(
-                out=q[:].rearrange("p h t -> p (h t)"), in_=st[k]["pr"][:], func=ACT.Sqrt, scale=1.0 / 256.0
-            )
+            j, t = chunks[k]
+            q = small.tile([P, t], F32, name="q", tag="q")
+            nc.scalar.activation(out=q[:], in_=st[k]["ss"][:], func=ACT.Sqrt, scale=1.0 / 256.0)
             st[k]["q"] = q
 
         def denom(k):
-            if not ok(k):
+            if k < 0 or k >= n:
                 return
-            dn = small.tile([P, 2, T], F32, name="dn", tag="dn")
-            nc.vector.tensor_tensor(out=dn[:], in0=st[k]["q"][:], in1=md160[:, :, k * T:(k + 1) * T], op=ALU.add)
+            j, t = chunks[k]
+            dn = small.tile([P, t], F32, name="dn", tag="dn")
+            nc.vector.tensor_tensor(out=dn[:], in0=st[k]["q"][:], in1=md160[:, j:j + t], op=ALU.add)
             st[k]["dn"] = dn
 
         def recip(k):
-            if not ok(k):
+            if k < 0 or k >= n:
                 return
-            f = small.tile([P, 2, T], F32, name="f", tag="f")
+            j, t = chunks[k]
+            f = small.tile([P, t], F32, name="f", tag="f")
             nc.vector.reciprocal(out=f[:], in_=st[k]["dn"][:])
             st[k]["f"] = f
 
         def scale_and_transpose(k):
-            if not ok(k):
+            if k < 0 or k >= n:
                 return
+            j, t = chunks[k]
             f = st[k]["f"]
-            y = work.tile([P, 2, T, HD], BF16, name="y", tag="y")
-            for t in range(T):
-                for h in range(2):
-                    nc.vector.tensor_scalar(
-                        out=y[:, h, t, :], in0=st[k]["s"][:, h, t, :], scalar1=f[:, h, t:t + 1], scalar2=None, op0=ALU.mult
-                    )
+            y = work.tile([P, t, D], BF16, name="y", tag="y")
+            for u in range(t):
+                nc.vector.tensor_scalar(
+                    out=y[:, u, :], in0=st[k]["s"][:, u, :], scalar1=f[:, u:u + 1], scalar2=None, op0=ALU.mult
+                )
             banks = []
-            for t0 in range(0, T, 2):
-                tp = ps_t.tile([P, 2, R, 2, 2, 2], BF16, name="tp", tag="tp")
-                for e in range(2):
-                    for h in range(2):
-                        for v in range(2):
-                            nc.tensor.transpose(tp[:, e, :, h, v, :], y[:, h, t0 + e, v * P:(v + 1) * P], ident[:])
-                banks.append(tp)
+            for u0 in range(0, t, 2):
+                w = min(2, t - u0)
+                tp = ps_t.tile([P, 2, KB, P], BF16, name="tp", tag="tp")
+                for u in range(w):
+                    for b in range(KB):
+                        nc.tensor.transpose(tp[:, u, b, :], y[:, u0 + u, b * P:(b + 1) * P], ident[:])
+                banks.append((u0, w, tp))
             st[k]["banks"] = banks
 
-        def copy_banks(k):
-            if not ok(k):
+        def regroup(k):
+            if k < 0 or k >= n:
                 return
-            g = work.tile([P, T * D], BF16, name="g", tag="g", align_bytes=64)
-            for i, tp in enumerate(st[k]["banks"]):
-                nc.scalar.copy(out=g[:, i * 2 * D:(i + 1) * 2 * D], in_=tp[:].rearrange("p e r h v u -> p (e r h v u)"))
+            j, t = chunks[k]
+            g = work.tile([P, t, P, KB], BF16, name="g", tag="g", align_bytes=64)
+            for u0, w, tp in st[k]["banks"]:
+                nc.scalar.copy(out=g[:, u0:u0 + w, :, :], in_=tp[:, 0:w, :, :].rearrange("p u b r -> p u r b"))
             st[k]["g"] = g
 
         def quant_and_multiply(k):
-            if not ok(k):
+            if k < 0 or k >= n:
                 return
-            codes = work.tile([P, T * P], U32, name="codes", tag="codes", align_bytes=64)
-            scales = work.tile([P, T * P], U8, name="scales", tag="scales", align_bytes=64)
-            nc.vector.quantize_mx(out=codes[:].bitcast(FP8X4), scales=scales[:], in_=st[k]["g"][:])
-            acc = ps_o.tile([P, T, C], F32, name="acc", tag="acc")
-            for t in range(T):
+            j, t = chunks[k]
+            codes = work.tile([P, t * P], U32, name="codes", tag="codes", align_bytes=64)
+            scales = work.tile([P, t * P], U8, name="scales", tag="scales", align_bytes=64)
+            nc.vector.quantize_mx(
+                out=codes[:].bitcast(FP8X4), scales=scales[:], in_=st[k]["g"][:].rearrange("p t r b -> p (t r b)")
+            )
+            acc = ps_o.tile([P, 4, C], F32, name="acc", tag="acc")
+            for u in range(t):
                 nc.tensor.matmul_mx(
-                    out=acc[:, t, :],
-                    lhsT=codes[:, t * P:(t + 1) * P].bitcast(FP8X4),
-                    lhsT_scale=scales[:, t * P:(t + 1) * P],
+                    out=acc[:, u, :],
+                    lhsT=codes[:, u * P:(u + 1) * P].bitcast(FP8X4),
+                    lhsT_scale=scales[:, u * P:(u + 1) * P],
                     rhs=w_codes[:].bitcast(FP8X4),
                     rhs_scale=w_scales[:],
                     start=True,
@@ -239,39 +203,24 @@ def tile_metaembedding_classifier_pb_t_kernel(tc, x, infused_feature, min_dist, 
             st[k]["acc"] = acc
 
         def store(k):
-            if not ok(k):
+            if k < 0 or k >= n:
                 return
-            o = op.tile([P, T, C], F32, name="o", tag="o")
-            if k % 2 == 1:
-                nc.vector.tensor_copy(out=o[:], in_=st[k]["acc"][:])
-            else:
-                nc.scalar.copy(out=o[:], in_=st[k]["acc"][:])
-            nc.sync.dma_start(out=o_v[:, k * T:(k + 1) * T, :], in_=o[:])
+            j, t = chunks[k]
+            o = op.tile([P, t, C], F32, name="o", tag="o")
+            nc.vector.tensor_copy(out=o[:], in_=st[k]["acc"][:, 0:t, :])
+            nc.sync.dma_start(out=o_v[:, j:j + t, :], in_=o[:])
 
         for k in range(-1, n + 5):
-            if k % 2 == 1:
-                load((k + 5) // 2, 1)
+            store(k - 4)
+            load(k + 4)
             root(k - 1)
-            if k == 1:
-                w_root()
             add(k + 1, 0)
             denom(k - 1)
-            if k == 1:
-                w_recip()
             add(k + 1, 1)
             recip(k - 1)
             if k == 0:
-                scale_md()
-            if k == 1:
-                w_scale_and_transpose()
-            if k == 2:
                 quant_w()
             squares(k)
-            if k == 0:
-                w_square()
             quant_and_multiply(k - 3)
             scale_and_transpose(k - 1)
-            copy_banks(k - 2)
-            if k == 1:
-                w_copy()
-            store(k - 4)
+            regroup(k - 2)

@@ -72,7 +72,7 @@ def tile_metaembedding_classifier_pb_t_kernel(tc, x, infused_feature, min_dist, 
         nc.vector.memset(one[:], 1.0)
         warm = const.tile([P, 1], F32, name="warm")
         nc.scalar.activation(out=warm[:], in_=one[:], func=ACT.Sqrt)
-        ident = const.tile([P, P], BF16, name="ident")
+        ident = const.tile([P, P], F32, name="ident")
         make_identity(nc, ident[:])
 
         md160 = const.tile([P, NT], F32, name="md160")
@@ -87,17 +87,19 @@ def tile_metaembedding_classifier_pb_t_kernel(tc, x, infused_feature, min_dist, 
         nc.vector.reciprocal(out=rw[:], in_=nw[:])
         ew = const.tile([P, D], BF16, name="ew")
         nc.vector.tensor_scalar(out=ew[:], in0=w_sb[:], scalar1=rw[:, 0:1], scalar2=None, op0=ALU.mult)
-        tpw = ps_t.tile([P, 2, KB, P], BF16, name="tpw", tag="tp")
-        for b in range(KB):
-            nc.tensor.transpose(tpw[:, 0, b, :], ew[:, b * P:(b + 1) * P], ident[:])
-        gw = const.tile([P, P, KB], BF16, name="gw", align_bytes=64)
-        nc.scalar.copy(out=gw[:], in_=tpw[:, 0, :, :].rearrange("p b r -> p r b"))
+        tpw = ps_t.tile([P, 2, 2, P], F32, name="tpw", tag="tp")
+        for e in range(2):
+            nc.tensor.transpose(tpw[:, 0, e, :], ew[:].bitcast(F32)[:, e::2], ident[:])
+        gw = const.tile([P, P * KB], BF16, name="gw", align_bytes=64)
+        nc.scalar.copy(
+            out=gw[:].bitcast(F32).rearrange("p (r e) -> p r e", e=2), in_=tpw[:, 0, :, :].rearrange("p e r -> p r e")
+        )
         w_codes = const.tile([P, C], U32, name="w_codes", align_bytes=64)
         w_scales = const.tile([P, C], U8, name="w_scales", align_bytes=64)
 
         def quant_w():
             nc.vector.quantize_mx(
-                out=w_codes[:].bitcast(FP8X4), scales=w_scales[:], in_=gw[:].rearrange("p r b -> p (r b)")
+                out=w_codes[:].bitcast(FP8X4), scales=w_scales[:], in_=gw[:]
             )
 
         def add(k, half):
@@ -164,10 +166,11 @@ def tile_metaembedding_classifier_pb_t_kernel(tc, x, infused_feature, min_dist, 
             banks = []
             for u0 in range(0, t, 2):
                 w = min(2, t - u0)
-                tp = ps_t.tile([P, 2, KB, P], BF16, name="tp", tag="tp")
+                tp = ps_t.tile([P, 2, 2, P], F32, name="tp", tag="tp")
                 for u in range(w):
-                    for b in range(KB):
-                        nc.tensor.transpose(tp[:, u, b, :], y[:, u0 + u, b * P:(b + 1) * P], ident[:])
+                    words = y[:, u0 + u, :].bitcast(F32)
+                    for e in range(2):
+                        nc.tensor.transpose(tp[:, u, e, :], words[:, e::2], ident[:])
                 banks.append((u0, w, tp))
             st[k]["banks"] = banks
 
@@ -175,9 +178,10 @@ def tile_metaembedding_classifier_pb_t_kernel(tc, x, infused_feature, min_dist, 
             if k < 0 or k >= n:
                 return
             j, t = chunks[k]
-            g = work.tile([P, t, P, KB], BF16, name="g", tag="g", align_bytes=64)
+            g = work.tile([P, t * P * KB], BF16, name="g", tag="g", align_bytes=64)
+            g_words = g[:].bitcast(F32).rearrange("p (u r e) -> p u r e", u=t, e=2)
             for u0, w, tp in st[k]["banks"]:
-                nc.scalar.copy(out=g[:, u0:u0 + w, :, :], in_=tp[:, 0:w, :, :].rearrange("p u b r -> p u r b"))
+                nc.scalar.copy(out=g_words[:, u0:u0 + w, :, :], in_=tp[:, 0:w, :, :].rearrange("p u e r -> p u r e"))
             st[k]["g"] = g
 
         def quant_and_multiply(k):
@@ -187,7 +191,7 @@ def tile_metaembedding_classifier_pb_t_kernel(tc, x, infused_feature, min_dist, 
             codes = work.tile([P, t * P], U32, name="codes", tag="codes", align_bytes=64)
             scales = work.tile([P, t * P], U8, name="scales", tag="scales", align_bytes=64)
             nc.vector.quantize_mx(
-                out=codes[:].bitcast(FP8X4), scales=scales[:], in_=st[k]["g"][:].rearrange("p t r b -> p (t r b)")
+                out=codes[:].bitcast(FP8X4), scales=scales[:], in_=st[k]["g"][:]
             )
             acc = ps_o.tile([P, 4, C], F32, name="acc", tag="acc")
             for u in range(t):

@@ -211,7 +211,7 @@ def tile_metaembedding_classifier_pb_t_kernel(tc, x, infused_feature, min_dist, 
                 return
             j, t = chunks[k]
             o = op.tile([P, t, C], F32, name="o", tag="o")
-            nc.vector.tensor_copy(out=o[:], in_=st[k]["acc"][:, 0:t, :])
+            nc.scalar.copy(out=o[:], in_=st[k]["acc"][:, 0:t, :])
             nc.sync.dma_start(out=o_v[:, j:j + t, :], in_=o[:])
 
         for k in range(-1, n + 5):

@@ -18,7 +18,7 @@ NT = B // P
 FLOPS = 2 * B * D * C
 
 PIN = True
-SIZES = [4] * 24
+SIZES = [1, 1, 2] + [4] * 22 + [2, 1, 1]
 
 
 def tile_metaembedding_classifier_pb_t_kernel(tc, x, infused_feature, min_dist, W_cos, out):
@@ -49,11 +49,6 @@ def tile_metaembedding_classifier_pb_t_kernel(tc, x, infused_feature, min_dist, 
 
         st = {}
 
-        w_sb = const.tile([P, D], BF16, name="w_sb")
-        nc.sync.dma_start(out=w_sb[:], in_=W_cos)
-        md_sb = const.tile([P, NT], BF16, name="md_sb")
-        nc.sync.dma_start(out=md_sb[:], in_=md_v)
-
         def load(k):
             if k < 0 or k >= n:
                 return
@@ -65,7 +60,11 @@ def tile_metaembedding_classifier_pb_t_kernel(tc, x, infused_feature, min_dist, 
             st[k] = {"x": xt, "i": it}
 
         load(0)
+        w_sb = const.tile([P, D], BF16, name="w_sb")
+        nc.sync.dma_start(out=w_sb[:], in_=W_cos)
         load(1)
+        md_sb = const.tile([P, NT], BF16, name="md_sb")
+        nc.sync.dma_start(out=md_sb[:], in_=md_v)
         load(2)
 
         one = const.tile([P, 1], F32, name="one")
@@ -74,33 +73,39 @@ def tile_metaembedding_classifier_pb_t_kernel(tc, x, infused_feature, min_dist, 
         nc.scalar.activation(out=warm[:], in_=one[:], func=ACT.Sqrt)
         ident = const.tile([P, P], F32, name="ident")
         make_identity(nc, ident[:])
-
         md160 = const.tile([P, NT], F32, name="md160")
-        nc.vector.tensor_scalar(out=md160[:], in0=md_sb[:], scalar1=1.0 / 160.0, scalar2=None, op0=ALU.mult)
-
-        junk_w = work.tile([P, D], BF16, name="junk_w", tag="junk")
-        ssw = const.tile([P, 1], F32, name="ssw")
-        nc.scalar.activation(out=junk_w[:], in_=w_sb[:], func=ACT.Square, accum_out=ssw[:])
         nw = const.tile([P, 1], F32, name="nw")
-        nc.scalar.activation(out=nw[:], in_=ssw[:], func=ACT.Sqrt)
-        rw = const.tile([P, 1], F32, name="rw")
-        nc.vector.reciprocal(out=rw[:], in_=nw[:])
         ew = const.tile([P, D], BF16, name="ew")
-        nc.vector.tensor_scalar(out=ew[:], in0=w_sb[:], scalar1=rw[:, 0:1], scalar2=None, op0=ALU.mult)
-        tpw = ps_t.tile([P, 2, 2, P], F32, name="tpw", tag="tp")
-        for e in range(2):
-            nc.tensor.transpose(tpw[:, 0, e, :], ew[:].bitcast(F32)[:, e::2], ident[:])
         gw = const.tile([P, P * KB], BF16, name="gw", align_bytes=64)
-        nc.scalar.copy(
-            out=gw[:].bitcast(F32).rearrange("p (r e) -> p r e", e=2), in_=tpw[:, 0, :, :].rearrange("p e r -> p r e")
-        )
         w_codes = const.tile([P, C], U32, name="w_codes", align_bytes=64)
         w_scales = const.tile([P, C], U8, name="w_scales", align_bytes=64)
 
-        def quant_w():
-            nc.vector.quantize_mx(
-                out=w_codes[:].bitcast(FP8X4), scales=w_scales[:], in_=gw[:]
+        def scale_min_dist():
+            nc.vector.tensor_scalar(out=md160[:], in0=md_sb[:], scalar1=1.0 / 160.0, scalar2=None, op0=ALU.mult)
+
+        def norm_w():
+            junk_w = work.tile([P, D], BF16, name="junk_w", tag="junk")
+            ssw = const.tile([P, 1], F32, name="ssw")
+            nc.scalar.activation(out=junk_w[:], in_=w_sb[:], func=ACT.Square, accum_out=ssw[:])
+            nc.scalar.activation(out=nw[:], in_=ssw[:], func=ACT.Sqrt)
+
+        def scale_and_transpose_w():
+            rw = const.tile([P, 1], F32, name="rw")
+            nc.vector.reciprocal(out=rw[:], in_=nw[:])
+            nc.vector.tensor_scalar(out=ew[:], in0=w_sb[:], scalar1=rw[:, 0:1], scalar2=None, op0=ALU.mult)
+            tpw = ps_t.tile([P, 2, 2, P], F32, name="tpw", tag="tp")
+            for e in range(2):
+                nc.tensor.transpose(tpw[:, 0, e, :], ew[:].bitcast(F32)[:, e::2], ident[:])
+            st["w"] = tpw
+
+        def regroup_w():
+            nc.scalar.copy(
+                out=gw[:].bitcast(F32).rearrange("p (r e) -> p r e", e=2),
+                in_=st["w"][:, 0, :, :].rearrange("p e r -> p r e"),
             )
+
+        def quant_w():
+            nc.vector.quantize_mx(out=w_codes[:].bitcast(FP8X4), scales=w_scales[:], in_=gw[:])
 
         def add(k, half):
             if k < 0 or k >= n:
@@ -223,8 +228,16 @@ def tile_metaembedding_classifier_pb_t_kernel(tc, x, infused_feature, min_dist, 
             add(k + 1, 1)
             recip(k - 1)
             if k == 0:
+                scale_min_dist()
+            if k == 3:
                 quant_w()
             squares(k)
+            if k == 0:
+                norm_w()
             quant_and_multiply(k - 3)
             scale_and_transpose(k - 1)
+            if k == 1:
+                scale_and_transpose_w()
             regroup(k - 2)
+            if k == 2:
+                regroup_w()

@@ -18,7 +18,7 @@ NT = B // P
 FLOPS = 2 * B * D * C
 
 PIN = True
-SIZES = [1, 1, 2] + [4] * 22 + [2, 1, 1]
+SIZES = [1, 1, 1, 1, 2, 2] + [4] * 21 + [2, 1, 1]
 
 
 def tile_metaembedding_classifier_pb_t_kernel(tc, x, infused_feature, min_dist, W_cos, out):
@@ -40,8 +40,8 @@ def tile_metaembedding_classifier_pb_t_kernel(tc, x, infused_feature, min_dist, 
             ctx.enter_context(tc.manual_schedule())
         const = ctx.enter_context(tc.tile_pool(name="const", bufs=1))
         ld = ctx.enter_context(tc.tile_pool(name="ld", bufs=4))
-        sp = ctx.enter_context(tc.tile_pool(name="sp", bufs=4))
-        small = ctx.enter_context(tc.tile_pool(name="small", bufs=6))
+        sp = ctx.enter_context(tc.tile_pool(name="sp", bufs=7))
+        small = ctx.enter_context(tc.tile_pool(name="small", bufs=8))
         work = ctx.enter_context(tc.tile_pool(name="work", bufs=3))
         op = ctx.enter_context(tc.tile_pool(name="op", bufs=4))
         ps_t = ctx.enter_context(tc.psum_pool(name="ps_t", bufs=5))
@@ -107,22 +107,18 @@ def tile_metaembedding_classifier_pb_t_kernel(tc, x, infused_feature, min_dist, 
         def quant_w():
             nc.vector.quantize_mx(out=w_codes[:].bitcast(FP8X4), scales=w_scales[:], in_=gw[:])
 
-        def add(k, half):
+        def add(k):
             if k < 0 or k >= n:
                 return
             j, t = chunks[k]
-            if half == 0:
-                st[k]["s"] = sp.tile([P, t, D], F32, name="s", tag="s")
-            h = (t + 1) // 2
-            lo, hi = (0, h) if half == 0 else (h, t)
-            if lo == hi:
-                return
+            s = sp.tile([P, t, D], F32, name="s", tag="s")
             nc.vector.tensor_tensor(
-                out=st[k]["s"][:, lo:hi, :].rearrange("p t d -> p (t d)"),
-                in0=st[k]["x"][:, lo:hi, :].rearrange("p t d -> p (t d)"),
-                in1=st[k]["i"][:, lo:hi, :].rearrange("p t d -> p (t d)"),
+                out=s[:].rearrange("p t d -> p (t d)"),
+                in0=st[k]["x"][:].rearrange("p t d -> p (t d)"),
+                in1=st[k]["i"][:].rearrange("p t d -> p (t d)"),
                 op=ALU.add,
             )
+            st[k]["s"] = s
 
         def squares(k):
             if k < 0 or k >= n:
@@ -219,25 +215,24 @@ def tile_metaembedding_classifier_pb_t_kernel(tc, x, infused_feature, min_dist, 
             nc.scalar.copy(out=o[:], in_=st[k]["acc"][:, 0:t, :])
             nc.sync.dma_start(out=o_v[:, j:j + t, :], in_=o[:])
 
-        for k in range(-1, n + 5):
+        for k in range(-3, n + 5):
+            load(k + 6)
+            root(k + 1)
             store(k - 4)
-            load(k + 4)
-            root(k - 1)
-            add(k + 1, 0)
-            denom(k - 1)
-            add(k + 1, 1)
-            recip(k - 1)
-            if k == 0:
+            denom(k)
+            add(k + 3)
+            recip(k)
+            if k == -1:
                 scale_min_dist()
             if k == 3:
                 quant_w()
-            squares(k)
-            if k == 0:
+            squares(k + 2)
+            if k == -1:
                 norm_w()
             quant_and_multiply(k - 3)
             scale_and_transpose(k - 1)
-            if k == 1:
+            if k == 0:
                 scale_and_transpose_w()
             regroup(k - 2)
-            if k == 2:
+            if k == 1:
                 regroup_w()

@@ -13,17 +13,15 @@ ALU = mybir.AluOpType
 
 P = 128
 B, D, C = 12288, 512, 128
-KB = D // P
 NT = B // P
 FLOPS = 2 * B * D * C
 
-PIN = True
-SIZES = [1, 1, 1, 1, 2, 2] + [4] * 21 + [2, 1, 1]
+SIZES = [1] * 4 + [2] * 4 + [4] * 19 + [2] * 3 + [1] * 2
 
 
 def tile_metaembedding_classifier_pb_t_kernel(tc, x, infused_feature, min_dist, W_cos, out):
     nc = tc.nc
-    assert sum(SIZES) == NT
+    assert sum(SIZES) == NT and len(SIZES) % 2 == 0
     x_v = x.rearrange("(p j) d -> p j d", p=P)
     i_v = infused_feature.rearrange("(p j) d -> p j d", p=P)
     o_v = out.rearrange("(p j) c -> p j c", p=P)
@@ -36,13 +34,12 @@ def tile_metaembedding_classifier_pb_t_kernel(tc, x, infused_feature, min_dist, 
     n = len(chunks)
 
     with ExitStack() as ctx:
-        if PIN:
-            ctx.enter_context(tc.manual_schedule())
+        ctx.enter_context(tc.manual_schedule())
         const = ctx.enter_context(tc.tile_pool(name="const", bufs=1))
         ld = ctx.enter_context(tc.tile_pool(name="ld", bufs=4))
         sp = ctx.enter_context(tc.tile_pool(name="sp", bufs=7))
-        small = ctx.enter_context(tc.tile_pool(name="small", bufs=8))
-        work = ctx.enter_context(tc.tile_pool(name="work", bufs=3))
+        small = ctx.enter_context(tc.tile_pool(name="small", bufs=4))
+        work = ctx.enter_context(tc.tile_pool(name="work", bufs=4))
         op = ctx.enter_context(tc.tile_pool(name="op", bufs=4))
         ps_t = ctx.enter_context(tc.psum_pool(name="ps_t", bufs=5))
         ps_o = ctx.enter_context(tc.psum_pool(name="ps_o", bufs=3))
@@ -57,7 +54,8 @@ def tile_metaembedding_classifier_pb_t_kernel(tc, x, infused_feature, min_dist, 
             nc.sync.dma_start(out=xt[:], in_=x_v[:, j:j + t, :])
             it = ld.tile([P, t, D], BF16, name="it", tag="it")
             nc.sync.dma_start(out=it[:], in_=i_v[:, j:j + t, :])
-            st[k] = {"x": xt, "i": it}
+            st["x", k] = xt
+            st["i", k] = it
 
         load(0)
         w_sb = const.tile([P, D], BF16, name="w_sb")
@@ -74,38 +72,37 @@ def tile_metaembedding_classifier_pb_t_kernel(tc, x, infused_feature, min_dist, 
         ident = const.tile([P, P], F32, name="ident")
         make_identity(nc, ident[:])
         md160 = const.tile([P, NT], F32, name="md160")
+        ssw = const.tile([P, 1], F32, name="ssw")
         nw = const.tile([P, 1], F32, name="nw")
+        rw = const.tile([P, 1], F32, name="rw")
         ew = const.tile([P, D], BF16, name="ew")
-        gw = const.tile([P, P * KB], BF16, name="gw", align_bytes=64)
+        gw = const.tile([P, 4 * C], BF16, name="gw", align_bytes=64)
         w_codes = const.tile([P, C], U32, name="w_codes", align_bytes=64)
         w_scales = const.tile([P, C], U8, name="w_scales", align_bytes=64)
 
-        def scale_min_dist():
-            nc.vector.tensor_scalar(out=md160[:], in0=md_sb[:], scalar1=1.0 / 160.0, scalar2=None, op0=ALU.mult)
-
-        def norm_w():
-            junk_w = work.tile([P, D], BF16, name="junk_w", tag="junk")
-            ssw = const.tile([P, 1], F32, name="ssw")
-            nc.scalar.activation(out=junk_w[:], in_=w_sb[:], func=ACT.Square, accum_out=ssw[:])
-            nc.scalar.activation(out=nw[:], in_=ssw[:], func=ACT.Sqrt)
-
-        def scale_and_transpose_w():
-            rw = const.tile([P, 1], F32, name="rw")
-            nc.vector.reciprocal(out=rw[:], in_=nw[:])
-            nc.vector.tensor_scalar(out=ew[:], in0=w_sb[:], scalar1=rw[:, 0:1], scalar2=None, op0=ALU.mult)
-            tpw = ps_t.tile([P, 2, 2, P], F32, name="tpw", tag="tp")
-            for e in range(2):
-                nc.tensor.transpose(tpw[:, 0, e, :], ew[:].bitcast(F32)[:, e::2], ident[:])
-            st["w"] = tpw
-
-        def regroup_w():
-            nc.scalar.copy(
-                out=gw[:].bitcast(F32).rearrange("p (r e) -> p r e", e=2),
-                in_=st["w"][:, 0, :, :].rearrange("p e r -> p r e"),
-            )
-
-        def quant_w():
-            nc.vector.quantize_mx(out=w_codes[:].bitcast(FP8X4), scales=w_scales[:], in_=gw[:])
+        def weights(k):
+            if k == -3:
+                junk_w = const.tile([P, D], F32, name="junk_w")
+                nc.vector.scalar_tensor_tensor(
+                    out=junk_w[:], in0=w_sb[:], scalar=1.0, in1=w_sb[:], op0=ALU.mult, op1=ALU.mult, accum_out=ssw[:]
+                )
+                nc.scalar.activation(out=nw[:], in_=ssw[:], func=ACT.Sqrt)
+            if k == -2:
+                nc.vector.tensor_scalar(out=md160[:], in0=md_sb[:], scalar1=1.0 / 160.0, scalar2=None, op0=ALU.mult)
+                nc.vector.reciprocal(out=rw[:], in_=nw[:])
+            if k == -1:
+                nc.vector.tensor_scalar(out=ew[:], in0=w_sb[:], scalar1=rw[:, 0:1], scalar2=None, op0=ALU.mult)
+                tpw = ps_t.tile([P, 2, 2, P], F32, name="tpw", tag="tp")
+                for e in range(2):
+                    nc.tensor.transpose(tpw[:, 0, e, :], ew[:].bitcast(F32)[:, e::2], ident[:])
+                st["w"] = tpw
+            if k == 0:
+                nc.vector.tensor_copy(
+                    out=gw[:].bitcast(F32).rearrange("p (r e) -> p r e", e=2),
+                    in_=st["w"][:, 0, :, :].rearrange("p e r -> p r e"),
+                )
+            if k == 1:
+                nc.vector.quantize_mx(out=w_codes[:].bitcast(FP8X4), scales=w_scales[:], in_=gw[:])
 
         def add(k):
             if k < 0 or k >= n:
@@ -114,55 +111,63 @@ def tile_metaembedding_classifier_pb_t_kernel(tc, x, infused_feature, min_dist, 
             s = sp.tile([P, t, D], F32, name="s", tag="s")
             nc.vector.tensor_tensor(
                 out=s[:].rearrange("p t d -> p (t d)"),
-                in0=st[k]["x"][:].rearrange("p t d -> p (t d)"),
-                in1=st[k]["i"][:].rearrange("p t d -> p (t d)"),
+                in0=st["x", k][:].rearrange("p t d -> p (t d)"),
+                in1=st["i", k][:].rearrange("p t d -> p (t d)"),
                 op=ALU.add,
             )
-            st[k]["s"] = s
+            st["s", k] = s
 
-        def squares(k):
+        def squares(k, half):
             if k < 0 or k >= n:
                 return
             j, t = chunks[k]
-            ss = small.tile([P, t], F32, name="ss", tag="ss")
-            for u in range(t):
+            if k % 2 == 0 and half == 0:
+                ss_new = small.tile([P, t + chunks[k + 1][1]], F32, name="ss", tag="ss")
+                st["ss", k] = (ss_new, 0)
+                st["ss", k + 1] = (ss_new, t)
+            ss, c0 = st["ss", k]
+            mid = (t + 1) // 2
+            for u in (range(mid) if half == 0 else range(mid, t)):
                 junk = work.tile([P, D], BF16, name="junk", tag="junk")
-                nc.scalar.activation(out=junk[:], in_=st[k]["s"][:, u, :], func=ACT.Square, accum_out=ss[:, u:u + 1])
-            st[k]["ss"] = ss
+                nc.scalar.activation(
+                    out=junk[:], in_=st["s", k][:, u, :], func=ACT.Square, accum_out=ss[:, c0 + u:c0 + u + 1]
+                )
 
         def root(k):
-            if k < 0 or k >= n:
+            if k < 0 or k >= n or k % 2:
                 return
-            j, t = chunks[k]
+            t = chunks[k][1] + chunks[k + 1][1]
             q = small.tile([P, t], F32, name="q", tag="q")
-            nc.scalar.activation(out=q[:], in_=st[k]["ss"][:], func=ACT.Sqrt, scale=1.0 / 256.0)
-            st[k]["q"] = q
+            nc.scalar.activation(out=q[:], in_=st["ss", k][0][:], func=ACT.Sqrt, scale=1.0 / 256.0)
+            st["q", k] = q
 
         def denom(k):
-            if k < 0 or k >= n:
+            if k < 0 or k >= n or k % 2:
                 return
-            j, t = chunks[k]
+            j = chunks[k][0]
+            t = chunks[k][1] + chunks[k + 1][1]
             dn = small.tile([P, t], F32, name="dn", tag="dn")
-            nc.vector.tensor_tensor(out=dn[:], in0=st[k]["q"][:], in1=md160[:, j:j + t], op=ALU.add)
-            st[k]["dn"] = dn
+            nc.vector.tensor_tensor(out=dn[:], in0=st["q", k][:], in1=md160[:, j:j + t], op=ALU.add)
+            st["dn", k] = dn
 
         def recip(k):
-            if k < 0 or k >= n:
+            if k < 0 or k >= n or k % 2:
                 return
-            j, t = chunks[k]
+            t = chunks[k][1] + chunks[k + 1][1]
             f = small.tile([P, t], F32, name="f", tag="f")
-            nc.vector.reciprocal(out=f[:], in_=st[k]["dn"][:])
-            st[k]["f"] = f
+            nc.vector.reciprocal(out=f[:], in_=st["dn", k][:])
+            st["f", k] = (f, 0)
+            st["f", k + 1] = (f, chunks[k][1])
 
         def scale_and_transpose(k):
             if k < 0 or k >= n:
                 return
             j, t = chunks[k]
-            f = st[k]["f"]
+            f, c0 = st["f", k]
             y = work.tile([P, t, D], BF16, name="y", tag="y")
             for u in range(t):
                 nc.vector.tensor_scalar(
-                    out=y[:, u, :], in0=st[k]["s"][:, u, :], scalar1=f[:, u:u + 1], scalar2=None, op0=ALU.mult
+                    out=y[:, u, :], in0=st["s", k][:, u, :], scalar1=f[:, c0 + u:c0 + u + 1], scalar2=None, op0=ALU.mult
                 )
             banks = []
             for u0 in range(0, t, 2):
@@ -173,17 +178,18 @@ def tile_metaembedding_classifier_pb_t_kernel(tc, x, infused_feature, min_dist, 
                     for e in range(2):
                         nc.tensor.transpose(tp[:, u, e, :], words[:, e::2], ident[:])
                 banks.append((u0, w, tp))
-            st[k]["banks"] = banks
+            st["banks", k] = banks
 
-        def regroup(k):
+        def regroup(k, half):
             if k < 0 or k >= n:
                 return
             j, t = chunks[k]
-            g = work.tile([P, t * P * KB], BF16, name="g", tag="g", align_bytes=64)
-            g_words = g[:].bitcast(F32).rearrange("p (u r e) -> p u r e", u=t, e=2)
-            for u0, w, tp in st[k]["banks"]:
+            if half == 0:
+                g_new = work.tile([P, t * 4 * P], BF16, name="g", tag="g", align_bytes=64)
+                st["g", k] = g_new
+            g_words = st["g", k][:].bitcast(F32).rearrange("p (u r e) -> p u r e", u=t, e=2)
+            for u0, w, tp in st["banks", k][half:half + 1]:
                 nc.scalar.copy(out=g_words[:, u0:u0 + w, :, :], in_=tp[:, 0:w, :, :].rearrange("p u e r -> p u r e"))
-            st[k]["g"] = g
 
         def quant_and_multiply(k):
             if k < 0 or k >= n:
@@ -191,9 +197,7 @@ def tile_metaembedding_classifier_pb_t_kernel(tc, x, infused_feature, min_dist, 
             j, t = chunks[k]
             codes = work.tile([P, t * P], U32, name="codes", tag="codes", align_bytes=64)
             scales = work.tile([P, t * P], U8, name="scales", tag="scales", align_bytes=64)
-            nc.vector.quantize_mx(
-                out=codes[:].bitcast(FP8X4), scales=scales[:], in_=st[k]["g"][:]
-            )
+            nc.vector.quantize_mx(out=codes[:].bitcast(FP8X4), scales=scales[:], in_=st["g", k][:])
             acc = ps_o.tile([P, 4, C], F32, name="acc", tag="acc")
             for u in range(t):
                 nc.tensor.matmul_mx(
@@ -205,34 +209,27 @@ def tile_metaembedding_classifier_pb_t_kernel(tc, x, infused_feature, min_dist, 
                     start=True,
                     stop=True,
                 )
-            st[k]["acc"] = acc
+            st["acc", k] = acc
 
         def store(k):
             if k < 0 or k >= n:
                 return
             j, t = chunks[k]
             o = op.tile([P, t, C], F32, name="o", tag="o")
-            nc.scalar.copy(out=o[:], in_=st[k]["acc"][:, 0:t, :])
+            nc.scalar.copy(out=o[:], in_=st["acc", k][:, 0:t, :])
             nc.sync.dma_start(out=o_v[:, j:j + t, :], in_=o[:])
 
-        for k in range(-3, n + 5):
-            load(k + 6)
+        for k in range(-4, n + 5):
+            load(k + 7)
             root(k + 1)
-            store(k - 4)
+            squares(k + 3, 0)
+            regroup(k - 2, 0)
+            squares(k + 3, 1)
+            regroup(k - 2, 1)
+            store(k - 5)
+            add(k + 4)
+            weights(k)
             denom(k)
-            add(k + 3)
+            quant_and_multiply(k - 4)
             recip(k)
-            if k == -1:
-                scale_min_dist()
-            if k == 3:
-                quant_w()
-            squares(k + 2)
-            if k == -1:
-                norm_w()
-            quant_and_multiply(k - 3)
             scale_and_transpose(k - 1)
-            if k == 0:
-                scale_and_transpose_w()
-            regroup(k - 2)
-            if k == 1:
-                regroup_w()

@@ -17,6 +17,7 @@ NT = B // P
 FLOPS = 2 * B * D * C
 
 SIZES = [1] * 4 + [2] * 4 + [4] * 19 + [2] * 3 + [1] * 2
+LOADS = [1, 1, 2] + [4] * 23
 
 
 def tile_metaembedding_classifier_pb_t_kernel(tc, x, infused_feature, min_dist, W_cos, out):
@@ -36,34 +37,40 @@ def tile_metaembedding_classifier_pb_t_kernel(tc, x, infused_feature, min_dist, 
     with ExitStack() as ctx:
         ctx.enter_context(tc.manual_schedule())
         const = ctx.enter_context(tc.tile_pool(name="const", bufs=1))
-        ld = ctx.enter_context(tc.tile_pool(name="ld", bufs=4))
+        ld = ctx.enter_context(tc.tile_pool(name="ld", bufs=6))
         sp = ctx.enter_context(tc.tile_pool(name="sp", bufs=7))
         small = ctx.enter_context(tc.tile_pool(name="small", bufs=4))
         work = ctx.enter_context(tc.tile_pool(name="work", bufs=4))
-        op = ctx.enter_context(tc.tile_pool(name="op", bufs=4))
+        op = ctx.enter_context(tc.tile_pool(name="op", bufs=8))
         ps_t = ctx.enter_context(tc.psum_pool(name="ps_t", bufs=5))
         ps_o = ctx.enter_context(tc.psum_pool(name="ps_o", bufs=3))
 
         st = {}
 
-        def load(k):
-            if k < 0 or k >= n:
-                return
-            j, t = chunks[k]
+        load_starts = [sum(LOADS[:m]) for m in range(len(LOADS))]
+
+        def load(m):
+            j, t = load_starts[m], LOADS[m]
             xt = ld.tile([P, t, D], BF16, name="xt", tag="xt")
             nc.sync.dma_start(out=xt[:], in_=x_v[:, j:j + t, :])
             it = ld.tile([P, t, D], BF16, name="it", tag="it")
             nc.sync.dma_start(out=it[:], in_=i_v[:, j:j + t, :])
-            st["x", k] = xt
-            st["i", k] = it
+            for u in range(t):
+                st["in", j + u] = (xt, it, u)
 
+        def load_up_to(k):
+            last = chunks[min(k, n - 1)]
+            while st["loads"] < len(LOADS) and load_starts[st["loads"]] < last[0] + last[1]:
+                load(st["loads"])
+                st["loads"] += 1
+
+        st["loads"] = 2
         load(0)
+        load(1)
         w_sb = const.tile([P, D], BF16, name="w_sb")
         nc.sync.dma_start(out=w_sb[:], in_=W_cos)
-        load(1)
         md_sb = const.tile([P, NT], BF16, name="md_sb")
         nc.sync.dma_start(out=md_sb[:], in_=md_v)
-        load(2)
 
         one = const.tile([P, 1], F32, name="one")
         nc.vector.memset(one[:], 1.0)
@@ -108,11 +115,12 @@ def tile_metaembedding_classifier_pb_t_kernel(tc, x, infused_feature, min_dist, 
             if k < 0 or k >= n:
                 return
             j, t = chunks[k]
+            xt, it, u = st["in", j]
             s = sp.tile([P, t, D], F32, name="s", tag="s")
             nc.vector.tensor_tensor(
                 out=s[:].rearrange("p t d -> p (t d)"),
-                in0=st["x", k][:].rearrange("p t d -> p (t d)"),
-                in1=st["i", k][:].rearrange("p t d -> p (t d)"),
+                in0=xt[:, u:u + t, :].rearrange("p t d -> p (t d)"),
+                in1=it[:, u:u + t, :].rearrange("p t d -> p (t d)"),
                 op=ALU.add,
             )
             st["s", k] = s
@@ -220,12 +228,12 @@ def tile_metaembedding_classifier_pb_t_kernel(tc, x, infused_feature, min_dist, 
             nc.sync.dma_start(out=o_v[:, j:j + t, :], in_=o[:])
 
         for k in range(-4, n + 5):
-            load(k + 7)
-            root(k + 1)
+            load_up_to(k + 8)
             squares(k + 3, 0)
             regroup(k - 2, 0)
             squares(k + 3, 1)
             regroup(k - 2, 1)
+            root(k + 2)
             store(k - 5)
             add(k + 4)
             weights(k)

@@ -18,11 +18,13 @@ FLOPS = 2 * B * D * C
 
 SIZES = [1] * 4 + [2] * 4 + [4] * 19 + [2] * 3 + [1] * 2
 LOADS = [1, 1, 2] + [4] * 23
+ON_TENSOR = range(8, 25, 8)
+G = 4
 
 
 def tile_metaembedding_classifier_pb_t_kernel(tc, x, infused_feature, min_dist, W_cos, out):
     nc = tc.nc
-    assert sum(SIZES) == NT and len(SIZES) % 2 == 0
+    assert sum(SIZES) == NT and len(SIZES) % G == 0
     x_v = x.rearrange("(p j) d -> p j d", p=P)
     i_v = infused_feature.rearrange("(p j) d -> p j d", p=P)
     o_v = out.rearrange("(p j) c -> p j c", p=P)
@@ -38,11 +40,12 @@ def tile_metaembedding_classifier_pb_t_kernel(tc, x, infused_feature, min_dist, 
         ctx.enter_context(tc.manual_schedule())
         const = ctx.enter_context(tc.tile_pool(name="const", bufs=1))
         ld = ctx.enter_context(tc.tile_pool(name="ld", bufs=6))
-        sp = ctx.enter_context(tc.tile_pool(name="sp", bufs=7))
+        sp = ctx.enter_context(tc.tile_pool(name="sp", bufs=9))
         small = ctx.enter_context(tc.tile_pool(name="small", bufs=4))
         work = ctx.enter_context(tc.tile_pool(name="work", bufs=4))
         op = ctx.enter_context(tc.tile_pool(name="op", bufs=8))
-        ps_t = ctx.enter_context(tc.psum_pool(name="ps_t", bufs=5))
+        ps_t = ctx.enter_context(tc.psum_pool(name="ps_t", bufs=4))
+        ps_s = ctx.enter_context(tc.psum_pool(name="ps_s", bufs=1))
         ps_o = ctx.enter_context(tc.psum_pool(name="ps_o", bufs=3))
 
         st = {}
@@ -78,6 +81,8 @@ def tile_metaembedding_classifier_pb_t_kernel(tc, x, infused_feature, min_dist, 
         nc.scalar.activation(out=warm[:], in_=one[:], func=ACT.Sqrt)
         ident = const.tile([P, P], F32, name="ident")
         make_identity(nc, ident[:])
+        ident_b = const.tile([P, P], BF16, name="ident_b")
+        make_identity(nc, ident_b[:])
         md160 = const.tile([P, NT], F32, name="md160")
         ssw = const.tile([P, 1], F32, name="ssw")
         nw = const.tile([P, 1], F32, name="nw")
@@ -87,28 +92,29 @@ def tile_metaembedding_classifier_pb_t_kernel(tc, x, infused_feature, min_dist, 
         w_codes = const.tile([P, C], U32, name="w_codes", align_bytes=64)
         w_scales = const.tile([P, C], U8, name="w_scales", align_bytes=64)
 
-        def weights(k):
-            if k == -3:
-                junk_w = const.tile([P, D], F32, name="junk_w")
-                nc.vector.scalar_tensor_tensor(
-                    out=junk_w[:], in0=w_sb[:], scalar=1.0, in1=w_sb[:], op0=ALU.mult, op1=ALU.mult, accum_out=ssw[:]
-                )
-                nc.scalar.activation(out=nw[:], in_=ssw[:], func=ACT.Sqrt)
+        def weights_on_scalar(k):
             if k == -2:
+                junk_w = work.tile([P, D], BF16, name="junk_w", tag="junk")
+                nc.scalar.activation(out=junk_w[:], in_=w_sb[:], func=ACT.Square, accum_out=ssw[:])
+            if k == -1:
+                nc.scalar.activation(out=nw[:], in_=ssw[:], func=ACT.Sqrt)
+            if k == 1:
+                nc.scalar.copy(
+                    out=gw[:].bitcast(F32).rearrange("p (r e) -> p r e", e=2),
+                    in_=st["w"][:, 0, :, :].rearrange("p e r -> p r e"),
+                )
+
+        def weights_on_vector(k):
+            if k == -1:
                 nc.vector.tensor_scalar(out=md160[:], in0=md_sb[:], scalar1=1.0 / 160.0, scalar2=None, op0=ALU.mult)
                 nc.vector.reciprocal(out=rw[:], in_=nw[:])
-            if k == -1:
+            if k == 0:
                 nc.vector.tensor_scalar(out=ew[:], in0=w_sb[:], scalar1=rw[:, 0:1], scalar2=None, op0=ALU.mult)
                 tpw = ps_t.tile([P, 2, 2, P], F32, name="tpw", tag="tp")
                 for e in range(2):
                     nc.tensor.transpose(tpw[:, 0, e, :], ew[:].bitcast(F32)[:, e::2], ident[:])
                 st["w"] = tpw
-            if k == 0:
-                nc.vector.tensor_copy(
-                    out=gw[:].bitcast(F32).rearrange("p (r e) -> p r e", e=2),
-                    in_=st["w"][:, 0, :, :].rearrange("p e r -> p r e"),
-                )
-            if k == 1:
+            if k == 2:
                 nc.vector.quantize_mx(out=w_codes[:].bitcast(FP8X4), scales=w_scales[:], in_=gw[:])
 
         def add(k):
@@ -116,56 +122,65 @@ def tile_metaembedding_classifier_pb_t_kernel(tc, x, infused_feature, min_dist, 
                 return
             j, t = chunks[k]
             xt, it, u = st["in", j]
+            v = t - 1 if k in ON_TENSOR else t
             s = sp.tile([P, t, D], F32, name="s", tag="s")
             nc.vector.tensor_tensor(
-                out=s[:].rearrange("p t d -> p (t d)"),
-                in0=xt[:, u:u + t, :].rearrange("p t d -> p (t d)"),
-                in1=it[:, u:u + t, :].rearrange("p t d -> p (t d)"),
+                out=s[:, 0:v, :].rearrange("p t d -> p (t d)"),
+                in0=xt[:, u:u + v, :].rearrange("p t d -> p (t d)"),
+                in1=it[:, u:u + v, :].rearrange("p t d -> p (t d)"),
                 op=ALU.add,
             )
-            st["s", k] = s
+            st["s", k] = [s[:, w, :] for w in range(v)]
+            if v < t:
+                s_ps = ps_s.tile([P, D], F32, name="s_ps", tag="s_ps")
+                nc.tensor.matmul(s_ps[:], lhsT=ident_b[:], rhs=xt[:, u + v, :], start=True, stop=False)
+                nc.tensor.matmul(s_ps[:], lhsT=ident_b[:], rhs=it[:, u + v, :], start=False, stop=True)
+                st["s", k].append(s_ps[:])
+
+        def group_size(k):
+            return chunks[k + G - 1][0] + chunks[k + G - 1][1] - chunks[k][0]
 
         def squares(k, half):
             if k < 0 or k >= n:
                 return
             j, t = chunks[k]
-            if k % 2 == 0 and half == 0:
-                ss_new = small.tile([P, t + chunks[k + 1][1]], F32, name="ss", tag="ss")
-                st["ss", k] = (ss_new, 0)
-                st["ss", k + 1] = (ss_new, t)
+            if k % G == 0 and half == 0:
+                ss_new = small.tile([P, group_size(k)], F32, name="ss", tag="ss")
+                for m in range(k, k + G):
+                    st["ss", m] = (ss_new, chunks[m][0] - j)
             ss, c0 = st["ss", k]
             mid = (t + 1) // 2
             for u in (range(mid) if half == 0 else range(mid, t)):
                 junk = work.tile([P, D], BF16, name="junk", tag="junk")
                 nc.scalar.activation(
-                    out=junk[:], in_=st["s", k][:, u, :], func=ACT.Square, accum_out=ss[:, c0 + u:c0 + u + 1]
+                    out=junk[:], in_=st["s", k][u], func=ACT.Square, accum_out=ss[:, c0 + u:c0 + u + 1]
                 )
 
         def root(k):
-            if k < 0 or k >= n or k % 2:
+            if k < 0 or k >= n or k % G:
                 return
-            t = chunks[k][1] + chunks[k + 1][1]
+            t = group_size(k)
             q = small.tile([P, t], F32, name="q", tag="q")
             nc.scalar.activation(out=q[:], in_=st["ss", k][0][:], func=ACT.Sqrt, scale=1.0 / 256.0)
             st["q", k] = q
 
         def denom(k):
-            if k < 0 or k >= n or k % 2:
+            if k < 0 or k >= n or k % G:
                 return
             j = chunks[k][0]
-            t = chunks[k][1] + chunks[k + 1][1]
+            t = group_size(k)
             dn = small.tile([P, t], F32, name="dn", tag="dn")
             nc.vector.tensor_tensor(out=dn[:], in0=st["q", k][:], in1=md160[:, j:j + t], op=ALU.add)
             st["dn", k] = dn
 
         def recip(k):
-            if k < 0 or k >= n or k % 2:
+            if k < 0 or k >= n or k % G:
                 return
-            t = chunks[k][1] + chunks[k + 1][1]
+            t = group_size(k)
             f = small.tile([P, t], F32, name="f", tag="f")
             nc.vector.reciprocal(out=f[:], in_=st["dn", k][:])
-            st["f", k] = (f, 0)
-            st["f", k + 1] = (f, chunks[k][1])
+            for m in range(k, k + G):
+                st["f", m] = (f, chunks[m][0] - chunks[k][0])
 
         def scale_and_transpose(k):
             if k < 0 or k >= n:
@@ -175,7 +190,7 @@ def tile_metaembedding_classifier_pb_t_kernel(tc, x, infused_feature, min_dist, 
             y = work.tile([P, t, D], BF16, name="y", tag="y")
             for u in range(t):
                 nc.vector.tensor_scalar(
-                    out=y[:, u, :], in0=st["s", k][:, u, :], scalar1=f[:, c0 + u:c0 + u + 1], scalar2=None, op0=ALU.mult
+                    out=y[:, u, :], in0=st["s", k][u], scalar1=f[:, c0 + u:c0 + u + 1], scalar2=None, op0=ALU.mult
                 )
             banks = []
             for u0 in range(0, t, 2):
@@ -227,16 +242,17 @@ def tile_metaembedding_classifier_pb_t_kernel(tc, x, infused_feature, min_dist, 
             nc.scalar.copy(out=o[:], in_=st["acc", k][:, 0:t, :])
             nc.sync.dma_start(out=o_v[:, j:j + t, :], in_=o[:])
 
-        for k in range(-4, n + 5):
-            load_up_to(k + 8)
-            squares(k + 3, 0)
+        for k in range(-6, n + 5):
+            load_up_to(k + 10)
+            squares(k + 5, 0)
             regroup(k - 2, 0)
-            squares(k + 3, 1)
+            squares(k + 5, 1)
             regroup(k - 2, 1)
             root(k + 2)
+            weights_on_scalar(k)
             store(k - 5)
-            add(k + 4)
-            weights(k)
+            add(k + 6)
+            weights_on_vector(k)
             denom(k)
             quant_and_multiply(k - 4)
             recip(k)

@@ -17,7 +17,7 @@ NT = B // P
 FLOPS = 2 * B * D * C
 
 SIZES = [1] * 4 + [2] * 4 + [4] * 19 + [2] * 3 + [1] * 2
-LOADS = [1, 1, 2] + [4] * 23
+LOADS = [1, 1, 2, 2, 2] + [4] * 22
 ON_TENSOR = range(8, 25, 8)
 G = 4
 
@@ -39,7 +39,7 @@ def tile_metaembedding_classifier_pb_t_kernel(tc, x, infused_feature, min_dist, 
     with ExitStack() as ctx:
         ctx.enter_context(tc.manual_schedule())
         const = ctx.enter_context(tc.tile_pool(name="const", bufs=1))
-        ld = ctx.enter_context(tc.tile_pool(name="ld", bufs=6))
+        ld = ctx.enter_context(tc.tile_pool(name="ld", bufs=7))
         sp = ctx.enter_context(tc.tile_pool(name="sp", bufs=9))
         small = ctx.enter_context(tc.tile_pool(name="small", bufs=4))
         work = ctx.enter_context(tc.tile_pool(name="work", bufs=4))
@@ -92,29 +92,29 @@ def tile_metaembedding_classifier_pb_t_kernel(tc, x, infused_feature, min_dist, 
         w_codes = const.tile([P, C], U32, name="w_codes", align_bytes=64)
         w_scales = const.tile([P, C], U8, name="w_scales", align_bytes=64)
 
-        def weights_on_scalar(k):
-            if k == -2:
-                junk_w = work.tile([P, D], BF16, name="junk_w", tag="junk")
-                nc.scalar.activation(out=junk_w[:], in_=w_sb[:], func=ACT.Square, accum_out=ssw[:])
-            if k == -1:
-                nc.scalar.activation(out=nw[:], in_=ssw[:], func=ACT.Sqrt)
-            if k == 1:
-                nc.scalar.copy(
-                    out=gw[:].bitcast(F32).rearrange("p (r e) -> p r e", e=2),
-                    in_=st["w"][:, 0, :, :].rearrange("p e r -> p r e"),
-                )
-
         def weights_on_vector(k):
-            if k == -1:
+            if k == -4:
+                junk_w = const.tile([P, D], F32, name="junk_w")
+                nc.vector.scalar_tensor_tensor(
+                    out=junk_w[:], in0=w_sb[:], scalar=1.0, in1=w_sb[:], op0=ALU.mult, op1=ALU.mult, accum_out=ssw[:]
+                )
+            if k == -3:
+                nc.scalar.activation(out=nw[:], in_=ssw[:], func=ACT.Sqrt)
                 nc.vector.tensor_scalar(out=md160[:], in0=md_sb[:], scalar1=1.0 / 160.0, scalar2=None, op0=ALU.mult)
+            if k == -2:
                 nc.vector.reciprocal(out=rw[:], in_=nw[:])
-            if k == 0:
+            if k == -1:
                 nc.vector.tensor_scalar(out=ew[:], in0=w_sb[:], scalar1=rw[:, 0:1], scalar2=None, op0=ALU.mult)
                 tpw = ps_t.tile([P, 2, 2, P], F32, name="tpw", tag="tp")
                 for e in range(2):
                     nc.tensor.transpose(tpw[:, 0, e, :], ew[:].bitcast(F32)[:, e::2], ident[:])
                 st["w"] = tpw
-            if k == 2:
+            if k == 0:
+                nc.vector.tensor_copy(
+                    out=gw[:].bitcast(F32).rearrange("p (r e) -> p r e", e=2),
+                    in_=st["w"][:, 0, :, :].rearrange("p e r -> p r e"),
+                )
+            if k == 1:
                 nc.vector.quantize_mx(out=w_codes[:].bitcast(FP8X4), scales=w_scales[:], in_=gw[:])
 
         def add(k):
@@ -249,7 +249,6 @@ def tile_metaembedding_classifier_pb_t_kernel(tc, x, infused_feature, min_dist, 
             squares(k + 5, 1)
             regroup(k - 2, 1)
             root(k + 2)
-            weights_on_scalar(k)
             store(k - 5)
             add(k + 6)
             weights_on_vector(k)

from contextlib import ExitStack

import concourse.mybir as mybir
from concourse.masks import make_identity

BF16 = mybir.dt.bfloat16
F32 = mybir.dt.float32
U32 = mybir.dt.uint32
U8 = mybir.dt.uint8
FP8X4 = mybir.dt.float8_e4m3fn_x4
ACT = mybir.ActivationFunctionType
ALU = mybir.AluOpType

P = 128
B, D, C = 12288, 512, 128
NT = B // P
FLOPS = 2 * B * D * C

SIZES = [1] * 4 + [2] * 4 + [4] * 19 + [2] * 3 + [1] * 2
LOADS = [1, 1, 2, 2, 2] + [4] * 22
ON_TENSOR = range(8, 25, 8)
G = 4


def tile_metaembedding_classifier_pb_t_kernel(tc, x, infused_feature, min_dist, W_cos, out):
    nc = tc.nc
    assert sum(SIZES) == NT and len(SIZES) % G == 0
    x_v = x.rearrange("(p j) d -> p j d", p=P)
    i_v = infused_feature.rearrange("(p j) d -> p j d", p=P)
    o_v = out.rearrange("(p j) c -> p j c", p=P)
    md_v = min_dist.rearrange("(p j) o -> p (j o)", p=P)
    chunks = []
    j0 = 0
    for size in SIZES:
        chunks.append((j0, size))
        j0 += size
    n = len(chunks)

    with ExitStack() as ctx:
        ctx.enter_context(tc.manual_schedule())
        const = ctx.enter_context(tc.tile_pool(name="const", bufs=1))
        ld = ctx.enter_context(tc.tile_pool(name="ld", bufs=7))
        sp = ctx.enter_context(tc.tile_pool(name="sp", bufs=9))
        small = ctx.enter_context(tc.tile_pool(name="small", bufs=4))
        work = ctx.enter_context(tc.tile_pool(name="work", bufs=4))
        op = ctx.enter_context(tc.tile_pool(name="op", bufs=8))
        ps_t = ctx.enter_context(tc.psum_pool(name="ps_t", bufs=4))
        ps_s = ctx.enter_context(tc.psum_pool(name="ps_s", bufs=1))
        ps_o = ctx.enter_context(tc.psum_pool(name="ps_o", bufs=3))

        st = {}

        load_starts = [sum(LOADS[:m]) for m in range(len(LOADS))]

        def load(m):
            j, t = load_starts[m], LOADS[m]
            xt = ld.tile([P, t, D], BF16, name="xt", tag="xt")
            nc.sync.dma_start(out=xt[:], in_=x_v[:, j:j + t, :])
            it = ld.tile([P, t, D], BF16, name="it", tag="it")
            nc.sync.dma_start(out=it[:], in_=i_v[:, j:j + t, :])
            for u in range(t):
                st["in", j + u] = (xt, it, u)

        def load_up_to(k):
            last = chunks[min(k, n - 1)]
            while st["loads"] < len(LOADS) and load_starts[st["loads"]] < last[0] + last[1]:
                load(st["loads"])
                st["loads"] += 1

        st["loads"] = 2
        load(0)
        load(1)
        w_sb = const.tile([P, D], BF16, name="w_sb")
        nc.sync.dma_start(out=w_sb[:], in_=W_cos)
        md_sb = const.tile([P, NT], BF16, name="md_sb")
        nc.sync.dma_start(out=md_sb[:], in_=md_v)

        one = const.tile([P, 1], F32, name="one")
        nc.vector.memset(one[:], 1.0)
        warm = const.tile([P, 1], F32, name="warm")
        nc.scalar.activation(out=warm[:], in_=one[:], func=ACT.Sqrt)
        ident = const.tile([P, P], F32, name="ident")
        make_identity(nc, ident[:])
        ident_b = const.tile([P, P], BF16, name="ident_b")
        make_identity(nc, ident_b[:])
        md160 = const.tile([P, NT], F32, name="md160")
        ssw = const.tile([P, 1], F32, name="ssw")
        nw = const.tile([P, 1], F32, name="nw")
        rw = const.tile([P, 1], F32, name="rw")
        ew = const.tile([P, D], BF16, name="ew")
        gw = const.tile([P, 4 * C], BF16, name="gw", align_bytes=64)
        w_codes = const.tile([P, C], U32, name="w_codes", align_bytes=64)
        w_scales = const.tile([P, C], U8, name="w_scales", align_bytes=64)

        def weights_on_vector(k):
            if k == -4:
                junk_w = const.tile([P, D], F32, name="junk_w")
                nc.vector.scalar_tensor_tensor(
                    out=junk_w[:], in0=w_sb[:], scalar=1.0, in1=w_sb[:], op0=ALU.mult, op1=ALU.mult, accum_out=ssw[:]
                )
            if k == -3:
                nc.scalar.activation(out=nw[:], in_=ssw[:], func=ACT.Sqrt)
                nc.vector.tensor_scalar(out=md160[:], in0=md_sb[:], scalar1=1.0 / 160.0, scalar2=None, op0=ALU.mult)
            if k == -2:
                nc.vector.reciprocal(out=rw[:], in_=nw[:])
            if k == -1:
                nc.vector.tensor_scalar(out=ew[:], in0=w_sb[:], scalar1=rw[:, 0:1], scalar2=None, op0=ALU.mult)
                tpw = ps_t.tile([P, 2, 2, P], F32, name="tpw", tag="tp")
                for e in range(2):
                    nc.tensor.transpose(tpw[:, 0, e, :], ew[:].bitcast(F32)[:, e::2], ident[:])
                st["w"] = tpw
            if k == 0:
                nc.vector.tensor_copy(
                    out=gw[:].bitcast(F32).rearrange("p (r e) -> p r e", e=2),
                    in_=st["w"][:, 0, :, :].rearrange("p e r -> p r e"),
                )
            if k == 1:
                nc.vector.quantize_mx(out=w_codes[:].bitcast(FP8X4), scales=w_scales[:], in_=gw[:])

        def add(k):
            if k < 0 or k >= n:
                return
            j, t = chunks[k]
            xt, it, u = st["in", j]
            v = t - 1 if k in ON_TENSOR else t
            s = sp.tile([P, t, D], F32, name="s", tag="s")
            nc.vector.tensor_tensor(
                out=s[:, 0:v, :].rearrange("p t d -> p (t d)"),
                in0=xt[:, u:u + v, :].rearrange("p t d -> p (t d)"),
                in1=it[:, u:u + v, :].rearrange("p t d -> p (t d)"),
                op=ALU.add,
            )
            st["s", k] = [s[:, w, :] for w in range(v)]
            if v < t:
                s_ps = ps_s.tile([P, D], F32, name="s_ps", tag="s_ps")
                nc.tensor.matmul(s_ps[:], lhsT=ident_b[:], rhs=xt[:, u + v, :], start=True, stop=False)
                nc.tensor.matmul(s_ps[:], lhsT=ident_b[:], rhs=it[:, u + v, :], start=False, stop=True)
                st["s", k].append(s_ps[:])

        def group_size(k):
            return chunks[k + G - 1][0] + chunks[k + G - 1][1] - chunks[k][0]

        def squares(k, half):
            if k < 0 or k >= n:
                return
            j, t = chunks[k]
            if k % G == 0 and half == 0:
                ss_new = small.tile([P, group_size(k)], F32, name="ss", tag="ss")
                for m in range(k, k + G):
                    st["ss", m] = (ss_new, chunks[m][0] - j)
            ss, c0 = st["ss", k]
            mid = (t + 1) // 2
            for u in (range(mid) if half == 0 else range(mid, t)):
                junk = work.tile([P, D], BF16, name="junk", tag="junk")
                nc.scalar.activation(
                    out=junk[:], in_=st["s", k][u], func=ACT.Square, accum_out=ss[:, c0 + u:c0 + u + 1]
                )

        def root(k):
            if k < 0 or k >= n or k % G:
                return
            t = group_size(k)
            q = small.tile([P, t], F32, name="q", tag="q")
            nc.scalar.activation(out=q[:], in_=st["ss", k][0][:], func=ACT.Sqrt, scale=1.0 / 256.0)
            st["q", k] = q

        def denom(k):
            if k < 0 or k >= n or k % G:
                return
            j = chunks[k][0]
            t = group_size(k)
            dn = small.tile([P, t], F32, name="dn", tag="dn")
            nc.vector.tensor_tensor(out=dn[:], in0=st["q", k][:], in1=md160[:, j:j + t], op=ALU.add)
            st["dn", k] = dn

        def recip(k):
            if k < 0 or k >= n or k % G:
                return
            t = group_size(k)
            f = small.tile([P, t], F32, name="f", tag="f")
            nc.vector.reciprocal(out=f[:], in_=st["dn", k][:])
            for m in range(k, k + G):
                st["f", m] = (f, chunks[m][0] - chunks[k][0])

        def scale_and_transpose(k):
            if k < 0 or k >= n:
                return
            j, t = chunks[k]
            f, c0 = st["f", k]
            y = work.tile([P, t, D], BF16, name="y", tag="y")
            for u in range(t):
                nc.vector.tensor_scalar(
                    out=y[:, u, :], in0=st["s", k][u], scalar1=f[:, c0 + u:c0 + u + 1], scalar2=None, op0=ALU.mult
                )
            banks = []
            for u0 in range(0, t, 2):
                w = min(2, t - u0)
                tp = ps_t.tile([P, 2, 2, P], F32, name="tp", tag="tp")
                for u in range(w):
                    words = y[:, u0 + u, :].bitcast(F32)
                    for e in range(2):
                        nc.tensor.transpose(tp[:, u, e, :], words[:, e::2], ident[:])
                banks.append((u0, w, tp))
            st["banks", k] = banks

        def regroup(k, half):
            if k < 0 or k >= n:
                return
            j, t = chunks[k]
            if half == 0:
                g_new = work.tile([P, t * 4 * P], BF16, name="g", tag="g", align_bytes=64)
                st["g", k] = g_new
            g_words = st["g", k][:].bitcast(F32).rearrange("p (u r e) -> p u r e", u=t, e=2)
            for u0, w, tp in st["banks", k][half:half + 1]:
                nc.scalar.copy(out=g_words[:, u0:u0 + w, :, :], in_=tp[:, 0:w, :, :].rearrange("p u e r -> p u r e"))

        def quant_and_multiply(k):
            if k < 0 or k >= n:
                return
            j, t = chunks[k]
            codes = work.tile([P, t * P], U32, name="codes", tag="codes", align_bytes=64)
            scales = work.tile([P, t * P], U8, name="scales", tag="scales", align_bytes=64)
            nc.vector.quantize_mx(out=codes[:].bitcast(FP8X4), scales=scales[:], in_=st["g", k][:])
            acc = ps_o.tile([P, 4, C], F32, name="acc", tag="acc")
            for u in range(t):
                nc.tensor.matmul_mx(
                    out=acc[:, u, :],
                    lhsT=codes[:, u * P:(u + 1) * P].bitcast(FP8X4),
                    lhsT_scale=scales[:, u * P:(u + 1) * P],
                    rhs=w_codes[:].bitcast(FP8X4),
                    rhs_scale=w_scales[:],
                    start=True,
                    stop=True,
                )
            st["acc", k] = acc

        def store(k):
            if k < 0 or k >= n:
                return
            j, t = chunks[k]
            o = op.tile([P, t, C], F32, name="o", tag="o")
            nc.scalar.copy(out=o[:], in_=st["acc", k][:, 0:t, :])
            nc.sync.dma_start(out=o_v[:, j:j + t, :], in_=o[:])

        for k in range(-6, n + 5):
            load_up_to(k + 10)
            squares(k + 5, 0)
            regroup(k - 2, 0)
            squares(k + 5, 1)
            regroup(k - 2, 1)
            root(k + 2)
            store(k - 5)
            add(k + 6)
            weights_on_vector(k)
            denom(k)
            quant_and_multiply(k - 4)
            recip(k)
            scale_and_transpose(k - 1)
